import numpy as np
import ml_dtypes


def mxq(x, axis, fmt="e4m3"):
    dtype, down = {"e4m3": (ml_dtypes.float8_e4m3fn, 7), "e5m2": (ml_dtypes.float8_e5m2, 14)}[fmt]
    v = np.moveaxis(np.asarray(x, np.float32).astype(ml_dtypes.bfloat16).astype(np.float64), axis, -1)
    blocks = v.reshape(v.shape[:-1] + (-1, 32))
    amax = np.abs(blocks).max(-1, keepdims=True)
    byte = np.maximum(np.where(amax > 0, np.frexp(amax)[1] - 1 + 127, 0) - down, 1)
    scale = np.exp2(byte - 127.0)
    codes = (blocks / scale).astype(np.float32).astype(dtype).astype(np.float64)
    return np.moveaxis((codes * scale).reshape(v.shape), -1, axis)


WIDE = False


def mx_kscale(k):
    if not WIDE:
        return np.ones(k)
    levels = np.array([10, -10, 5, -5, 0])
    a = np.random.permutation(np.resize(levels, k // 512 * 4)).reshape(k // 512, 4)
    idx = np.arange(k)
    return np.exp2(a[idx // 512, idx % 128 // 32])


BF16 = ml_dtypes.bfloat16


def bf(x):
    return np.asarray(x, np.float32).astype(BF16)


def f64(x):
    return np.asarray(x).astype(np.float64)


E2M1 = np.array([0.0, 0.5, 1.0, 1.5, 2.0, 3.0, 4.0, 6.0, -0.0, -0.5, -1.0, -1.5, -2.0, -3.0, -4.0, -6.0])


def pack_weight(w, fmt):
    k, n = w.shape
    w = f64(bf(w)).reshape(k // 32, 32, n)
    amax = np.abs(w).max(1)
    if fmt == "e4m3":
        byte = np.frexp(amax)[1] - 1 + 127 - 7
    else:
        mant, ex = np.frexp(amax / 6.0)
        byte = np.where(mant > 0.5, ex, ex - 1) + 127
    byte = np.clip(np.where(amax > 0, byte, 1), 1, 254)
    scaled = (w * np.exp2(127.0 - byte)[:, None, :]).reshape(k, n).astype(np.float32)
    by_word = np.ascontiguousarray(scaled.reshape(k // 512, 128, 4, n).transpose(0, 1, 3, 2))
    if fmt == "e4m3":
        words = by_word.astype(ml_dtypes.float8_e4m3fn).view(np.uint8)
    else:
        c = by_word.astype(ml_dtypes.float4_e2m1fn).view(np.uint8) & 0xF
        words = c[..., 0::2] | (c[..., 1::2] << 4)
    return np.ascontiguousarray(words), np.ascontiguousarray(byte.astype(np.uint8).reshape(k // 512, 16, n))


def unpack_weight(words, scales, fmt):
    g, p, n, _ = words.shape
    if fmt == "e4m3":
        vals = np.ascontiguousarray(words).view(ml_dtypes.float8_e4m3fn).astype(np.float64)
    else:
        nib = np.empty((g, p, n, 4), np.uint8)
        nib[..., 0::2] = words & 0xF
        nib[..., 1::2] = words >> 4
        vals = E2M1[nib]
    vals = vals * np.repeat(np.exp2(scales.astype(np.float64) - 127.0), 8, axis=1)[..., None]
    return vals.transpose(0, 1, 3, 2).reshape(g * 512, n)


B, X, N, OS = 2048, 512, 2304, 256
H = N - OS


def setup_inputs():
    s, t = mx_kscale(X), mx_kscale(H)
    std0 = np.sqrt(2.0 / X)
    std1 = np.sqrt(2.0 / (X + H))
    row_scale = np.concatenate([std0 * t, np.full(OS, std1)])
    bias_scale = np.concatenate([t, np.ones(OS)])
    x = bf(np.random.standard_normal((B, X)) * s)
    w0_words, w0_scales = pack_weight((np.random.standard_normal((N, X)) * row_scale[:, None] / s).T, "e4m3")
    w1_words, w1_scales = pack_weight((np.random.standard_normal((OS, H)) * std1 / t).T, "e4m3")
    biases = bf(np.random.random(N) * bias_scale)
    return {"x": x,
            "w0_words": w0_words, "w0_scales": w0_scales,
            "w1_words": w1_words, "w1_scales": w1_scales,
            "biases": biases}


def reference(x, w0_words, w0_scales, w1_words, w1_scales, biases):
    n = w0_words.shape[2]
    os_ = w1_words.shape[2]
    z = (mxq(f64(x), 1, "e4m3") @ unpack_weight(w0_words, w0_scales, "e4m3")) + f64(biases)
    h = np.maximum(z[:, : n - os_], 0.0)
    return z[:, n - os_:] + (mxq(h, 1, "e4m3") @ unpack_weight(w1_words, w1_scales, "e4m3"))

@@ -1,0 +1,240 @@
+from contextlib import ExitStack
+
+import concourse.mybir as mybir
+from concourse.masks import make_identity
+
+F32 = mybir.dt.float32
+BF16 = mybir.dt.bfloat16
+I32 = mybir.dt.int32
+U32 = mybir.dt.uint32
+U8 = mybir.dt.uint8
+FP8X4 = mybir.dt.float8_e4m3fn_x4
+RELU = mybir.ActivationFunctionType.Relu
+ADD = mybir.AluOpType.add
+
+P = 128
+PACK = 4
+K_PASS = P * PACK
+
+TOKENS = 2048
+INPUTS = 512
+HIDDEN = 2048
+OUTPUTS = 256
+NODES = HIDDEN + OUTPUTS
+
+TOKEN_TILES = TOKENS // P
+BLOCK = 512
+ROUNDS = TOKENS // BLOCK
+TILES_PER_ROUND = BLOCK // P
+GROUPS = HIDDEN // K_PASS
+NODE_TILES_PER_GROUP = K_PASS // P
+WORDS_PER_NODE_TILE = P // PACK
+UNITS = ROUNDS * GROUPS
+
+REGROUP_LAG = 1
+QUANTISE_LAG = 2
+SECOND_LAG = 8
+
+FLOPS = 2 * TOKENS * INPUTS * NODES + 2 * TOKENS * HIDDEN * OUTPUTS
+
+
+def tile_spn_kernel(tc, x, w0_words, w0_scales, w1_words, w1_scales, biases, out):
+    nc = tc.nc
+    with ExitStack() as stack:
+        keep = stack.enter_context(tc.tile_pool(name="keep", bufs=1))
+        x_stage = stack.enter_context(tc.tile_pool(name="x_stage", bufs=2))
+        rows_pool = stack.enter_context(tc.tile_pool(name="rows", bufs=8))
+        planes_pool = stack.enter_context(tc.tile_pool(name="planes", bufs=4))
+        grouped_pool = stack.enter_context(tc.tile_pool(name="grouped", bufs=3))
+        hq_pool = stack.enter_context(tc.tile_pool(name="hq", bufs=3))
+        psum_x = stack.enter_context(tc.psum_pool(name="psum_x", bufs=2))
+        psum_z = stack.enter_context(tc.psum_pool(name="psum_z", bufs=4))
+        psum_o = stack.enter_context(tc.psum_pool(name="psum_o", bufs=2))
+        stack.enter_context(tc.manual_schedule())
+
+        x_sb = keep.tile([P, TOKEN_TILES, INPUTS], BF16)
+        xq_codes = keep.tile([P, TOKENS], U32, align_bytes=64)
+        xq_plane = keep.tile([P, TOKENS], U8, align_bytes=64)
+        w0_codes = keep.tile([P, NODES], U32, align_bytes=64)
+        w0_plane = keep.tile([P, NODES], U8, align_bytes=64)
+        w1_codes = keep.tile([P, GROUPS, OUTPUTS], U32, align_bytes=64)
+        w1_plane = keep.tile([P, GROUPS, OUTPUTS], U8, align_bytes=64)
+        bias_rows = keep.tile([P, P], BF16)
+        bias_col = keep.tile([P, HIDDEN // P], F32)
+        bias_out = keep.tile([P, OUTPUTS], BF16)
+        ident_f32 = keep.tile([P, P], F32)
+        ident_bf16 = keep.tile([P, P], BF16)
+        out_sb = keep.tile([P, TOKEN_TILES, OUTPUTS], F32)
+
+        nc.vector.memset(bias_rows[:], 0.0)
+        nc.vector.memset(w0_plane[:].bitcast(I32), 0)
+        nc.vector.memset(w1_plane[:].bitcast(I32), 0)
+        make_identity(nc, ident_f32[:])
+        make_identity(nc, ident_bf16[:])
+
+        x_by_tile = x.rearrange("(p a) k -> p a k", a=TOKEN_TILES)
+        out_by_tile = out.rearrange("(p a) o -> p a o", a=TOKEN_TILES)
+
+        def load_x(rnd):
+            tiles = slice(rnd * TILES_PER_ROUND, (rnd + 1) * TILES_PER_ROUND)
+            nc.sync.dma_start(out=x_sb[:, tiles, :], in_=x_by_tile[:, tiles, :])
+
+        load_x(0)
+        nc.sync.dma_start(
+            out=bias_rows[0 : HIDDEN // P, :], in_=biases[0:HIDDEN].rearrange("(j m) -> j m", m=P)
+        )
+        for quad in range(4):
+            nc.sync.dma_start(
+                out=w0_plane[32 * quad : 32 * quad + 4, :].bitcast(I32),
+                in_=w0_scales[0, 4 * quad : 4 * quad + 4, :].bitcast(I32),
+            )
+        w0_words_i32 = w0_words[0].rearrange("p n t -> p (n t)").bitcast(I32)
+        for first in range(0, NODES, K_PASS):
+            nodes = slice(first, min(first + K_PASS, NODES))
+            nc.sync.dma_start(out=w0_codes[:, nodes].bitcast(I32), in_=w0_words_i32[:, nodes])
+        load_x(1)
+        for quad in range(4):
+            nc.sync.dma_start(
+                out=w1_plane[32 * quad : 32 * quad + 4, :, :].bitcast(I32),
+                in_=w1_scales[:, 4 * quad : 4 * quad + 4, :].rearrange("g r n -> r g n").bitcast(I32),
+            )
+        nc.sync.dma_start(
+            out=w1_codes[:].bitcast(I32),
+            in_=w1_words.rearrange("g p n t -> p g (n t)").bitcast(I32),
+        )
+        nc.sync.dma_start(out=bias_out[:], in_=biases[HIDDEN:NODES].partition_broadcast(P))
+        load_x(2)
+        load_x(3)
+
+        def quantise_x(rnd):
+            x_grouped = x_stage.tile([P, BLOCK, PACK], BF16, align_bytes=64)
+            grouped_words = (
+                x_grouped[:]
+                .rearrange("p r t -> p (r t)")
+                .bitcast(F32)
+                .rearrange("p (i r u) -> p i r u", i=TILES_PER_ROUND, u=2)
+            )
+            banks = []
+            for pair in range(TILES_PER_ROUND // 2):
+                xt = psum_x.tile([P, 2, 2, P], F32, tag="xt")
+                banks.append(xt)
+                for i in range(2):
+                    a = rnd * TILES_PER_ROUND + 2 * pair + i
+                    words = x_sb[:, a, :].bitcast(F32).rearrange("p (q u) -> p u q", u=2)
+                    for u in range(2):
+                        nc.tensor.transpose(xt[:, i, u, :], words[:, u, :], ident_f32[:])
+            nc.scalar.copy(
+                out=grouped_words[:, 0:2, :, :], in_=banks[0][:].rearrange("p i u r -> p i r u")
+            )
+            nc.vector.tensor_copy(
+                out=grouped_words[:, 2:4, :, :], in_=banks[1][:].rearrange("p i u r -> p i r u")
+            )
+            cols = slice(rnd * BLOCK, (rnd + 1) * BLOCK)
+            nc.vector.quantize_mx(
+                out=xq_codes[:, cols].bitcast(FP8X4),
+                scales=xq_plane[:, cols],
+                in_=x_grouped[:].rearrange("p r t -> p (r t)"),
+            )
+
+        planes_of = {}
+        grouped_of = {}
+        hq_of = {}
+
+        def first_product(unit):
+            rnd, g = divmod(unit, GROUPS)
+            cols = slice(rnd * BLOCK, (rnd + 1) * BLOCK)
+            planes = planes_pool.tile([P, PACK, BLOCK], BF16)
+            planes_of[unit] = planes
+            for part in range(NODE_TILES_PER_GROUP):
+                j = g * NODE_TILES_PER_GROUP + part
+                nodes = slice(j * P, (j + 1) * P)
+                z = psum_z.tile([P, BLOCK], F32)
+                nc.tensor.matmul_mx(
+                    out=z[:],
+                    lhsT=w0_codes[:, nodes].bitcast(FP8X4),
+                    lhsT_scale=w0_plane[:, nodes],
+                    rhs=xq_codes[:, cols].bitcast(FP8X4),
+                    rhs_scale=xq_plane[:, cols],
+                    start=True,
+                    stop=True,
+                )
+                h_rows = rows_pool.tile([P, BLOCK], BF16)
+                nc.scalar.activation(
+                    out=h_rows[:], in_=z[:], func=RELU, bias=bias_col[:, j : j + 1], scale=1.0
+                )
+                first = part * WORDS_PER_NODE_TILE
+                nc.sync.dma_start(
+                    out=planes[first : first + WORDS_PER_NODE_TILE, :, :], in_=h_rows[:]
+                )
+
+        def regroup(unit):
+            grouped = grouped_pool.tile([P, BLOCK, PACK], BF16, align_bytes=64)
+            grouped_of[unit] = grouped
+            nc.vector.tensor_copy(
+                out=grouped[:].rearrange("p (c i) t -> p c t i", i=4),
+                in_=planes_of[unit][:].rearrange("p t (c i) -> p c t i", i=4),
+            )
+
+        def quantise_h(unit):
+            rnd, g = divmod(unit, GROUPS)
+            if g == 0:
+                hq_codes = hq_pool.tile([P, GROUPS, BLOCK], U32, align_bytes=64)
+                hq_plane = hq_pool.tile([P, GROUPS, BLOCK], U8, align_bytes=64)
+                hq_of[rnd] = (hq_codes, hq_plane)
+            hq_codes, hq_plane = hq_of[rnd]
+            nc.vector.quantize_mx(
+                out=hq_codes[:, g, :].bitcast(FP8X4),
+                scales=hq_plane[:, g, :],
+                in_=grouped_of[unit][:].rearrange("p r t -> p (r t)"),
+            )
+
+        def second_product(a):
+            rnd, i = divmod(a, TILES_PER_ROUND)
+            hq_codes, hq_plane = hq_of[rnd]
+            tile_cols = slice(i * P, (i + 1) * P)
+            acc = psum_o.tile([P, OUTPUTS], F32)
+            nc.tensor.matmul_mx(
+                out=acc[:],
+                lhsT=xq_codes[:, a * P : (a + 1) * P].bitcast(FP8X4),
+                lhsT_scale=xq_plane[:, a * P : (a + 1) * P],
+                rhs=w0_codes[:, HIDDEN:NODES].bitcast(FP8X4),
+                rhs_scale=w0_plane[:, HIDDEN:NODES],
+                start=True,
+                stop=False,
+            )
+            for g in range(GROUPS):
+                nc.tensor.matmul_mx(
+                    out=acc[:],
+                    lhsT=hq_codes[:, g, tile_cols].bitcast(FP8X4),
+                    lhsT_scale=hq_plane[:, g, tile_cols],
+                    rhs=w1_codes[:, g, :].bitcast(FP8X4),
+                    rhs_scale=w1_plane[:, g, :],
+                    start=False,
+                    stop=(g == GROUPS - 1),
+                )
+            nc.vector.tensor_tensor(out=out_sb[:, a, :], in0=acc[:], in1=bias_out[:], op=ADD)
+
+        def store(rnd):
+            tiles = slice(rnd * TILES_PER_ROUND, (rnd + 1) * TILES_PER_ROUND)
+            nc.sync.dma_start(out=out_by_tile[:, tiles, :], in_=out_sb[:, tiles, :])
+
+        quantise_x(0)
+        bias_ps = psum_x.tile([P, P], BF16, tag="xt")
+        nc.tensor.transpose(bias_ps[:], bias_rows[:], ident_bf16[:])
+        nc.vector.tensor_copy(out=bias_col[:], in_=bias_ps[:, 0 : HIDDEN // P])
+
+        for step in range(UNITS + SECOND_LAG + 1):
+            if step < UNITS:
+                first_product(step)
+            if 0 <= step - REGROUP_LAG < UNITS:
+                regroup(step - REGROUP_LAG)
+            if 0 <= step - QUANTISE_LAG < UNITS:
+                quantise_h(step - QUANTISE_LAG)
+            next_round = step // GROUPS + 1
+            if step % GROUPS == 1 and next_round < ROUNDS:
+                quantise_x(next_round)
+            if 0 <= step - SECOND_LAG < TOKEN_TILES:
+                second_product(step - SECOND_LAG)
+            stored, last = divmod(step - SECOND_LAG - 1, TILES_PER_ROUND)
+            if stored >= 0 and last == TILES_PER_ROUND - 1:
+                store(stored)

@@ -28,7 +28,6 @@ ROUNDS = TOKENS // BLOCK
 TILES_PER_ROUND = BLOCK // P
 GROUPS = HIDDEN // K_PASS
 NODE_TILES_PER_GROUP = K_PASS // P
-WORDS_PER_NODE_TILE = P // PACK
 UNITS = ROUNDS * GROUPS
 
 REGROUP_LAG = 1
@@ -55,8 +54,10 @@ def tile_spn_kernel(tc, x, w0_words, w0_scales, w1_words, w1_scales, biases, out
         x_sb = keep.tile([P, TOKEN_TILES, INPUTS], BF16)
         xq_codes = keep.tile([P, TOKENS], U32, align_bytes=64)
         xq_plane = keep.tile([P, TOKENS], U8, align_bytes=64)
-        w0_codes = keep.tile([P, NODES], U32, align_bytes=64)
-        w0_plane = keep.tile([P, NODES], U8, align_bytes=64)
+        w0_given_codes = keep.tile([P, NODES], U32, align_bytes=64)
+        w0_given_plane = keep.tile([P, NODES], U8, align_bytes=64)
+        w0_codes = keep.tile([P, HIDDEN], U32, align_bytes=64)
+        w0_plane = keep.tile([P, HIDDEN], U8, align_bytes=64)
         w1_codes = keep.tile([P, GROUPS, OUTPUTS], U32, align_bytes=64)
         w1_plane = keep.tile([P, GROUPS, OUTPUTS], U8, align_bytes=64)
         bias_rows = keep.tile([P, P], BF16)
@@ -67,7 +68,7 @@ def tile_spn_kernel(tc, x, w0_words, w0_scales, w1_words, w1_scales, biases, out
         out_sb = keep.tile([P, TOKEN_TILES, OUTPUTS], F32)
 
         nc.vector.memset(bias_rows[:], 0.0)
-        nc.vector.memset(w0_plane[:].bitcast(I32), 0)
+        nc.vector.memset(w0_given_plane[:].bitcast(I32), 0)
         nc.vector.memset(w1_plane[:].bitcast(I32), 0)
         make_identity(nc, ident_f32[:])
         make_identity(nc, ident_bf16[:])
@@ -80,18 +81,22 @@ def tile_spn_kernel(tc, x, w0_words, w0_scales, w1_words, w1_scales, biases, out
             nc.sync.dma_start(out=x_sb[:, tiles, :], in_=x_by_tile[:, tiles, :])
 
         load_x(0)
-        nc.sync.dma_start(
-            out=bias_rows[0 : HIDDEN // P, :], in_=biases[0:HIDDEN].rearrange("(j m) -> j m", m=P)
-        )
+        for g in range(GROUPS):
+            nc.sync.dma_start(
+                out=bias_rows[g * PACK : (g + 1) * PACK, :].rearrange("s (w c) -> s w c", c=PACK),
+                in_=biases[g * K_PASS : (g + 1) * K_PASS].rearrange(
+                    "(w s c) -> s w c", s=NODE_TILES_PER_GROUP, c=PACK
+                ),
+            )
         for quad in range(4):
             nc.sync.dma_start(
-                out=w0_plane[32 * quad : 32 * quad + 4, :].bitcast(I32),
+                out=w0_given_plane[32 * quad : 32 * quad + 4, :].bitcast(I32),
                 in_=w0_scales[0, 4 * quad : 4 * quad + 4, :].bitcast(I32),
             )
         w0_words_i32 = w0_words[0].rearrange("p n t -> p (n t)").bitcast(I32)
         for first in range(0, NODES, K_PASS):
             nodes = slice(first, min(first + K_PASS, NODES))
-            nc.sync.dma_start(out=w0_codes[:, nodes].bitcast(I32), in_=w0_words_i32[:, nodes])
+            nc.sync.dma_start(out=w0_given_codes[:, nodes].bitcast(I32), in_=w0_words_i32[:, nodes])
         load_x(1)
         for quad in range(4):
             nc.sync.dma_start(
@@ -136,6 +141,23 @@ def tile_spn_kernel(tc, x, w0_words, w0_scales, w1_words, w1_scales, biases, out
                 in_=x_grouped[:].rearrange("p r t -> p (r t)"),
             )
 
+        def reorder_w0_plane():
+            nc.vector.tensor_copy(
+                out=w0_plane[:].bitcast(I32).rearrange("p (g s w) -> p g s w", g=GROUPS, s=4),
+                in_=w0_given_plane[:, 0:HIDDEN]
+                .bitcast(I32)
+                .rearrange("p (g w s) -> p g s w", g=GROUPS, s=4),
+            )
+
+        def reorder_w0_codes(g):
+            nodes = slice(g * K_PASS, (g + 1) * K_PASS)
+            nc.vector.tensor_copy(
+                out=w0_codes[:, nodes].bitcast(I32).rearrange("p (s w c) -> p s w c", s=4, c=PACK),
+                in_=w0_given_codes[:, nodes]
+                .bitcast(I32)
+                .rearrange("p (w s c) -> p s w c", s=4, c=PACK),
+            )
+
         planes_of = {}
         grouped_of = {}
         hq_of = {}
@@ -162,10 +184,7 @@ def tile_spn_kernel(tc, x, w0_words, w0_scales, w1_words, w1_scales, biases, out
                 nc.scalar.activation(
                     out=h_rows[:], in_=z[:], func=RELU, bias=bias_col[:, j : j + 1], scale=1.0
                 )
-                first = part * WORDS_PER_NODE_TILE
-                nc.sync.dma_start(
-                    out=planes[first : first + WORDS_PER_NODE_TILE, :, :], in_=h_rows[:]
-                )
+                nc.sync.dma_start(out=planes[part:P:NODE_TILES_PER_GROUP, :, :], in_=h_rows[:])
 
         def regroup(unit):
             grouped = grouped_pool.tile([P, BLOCK, PACK], BF16, align_bytes=64)
@@ -197,8 +216,8 @@ def tile_spn_kernel(tc, x, w0_words, w0_scales, w1_words, w1_scales, biases, out
                 out=acc[:],
                 lhsT=xq_codes[:, a * P : (a + 1) * P].bitcast(FP8X4),
                 lhsT_scale=xq_plane[:, a * P : (a + 1) * P],
-                rhs=w0_codes[:, HIDDEN:NODES].bitcast(FP8X4),
-                rhs_scale=w0_plane[:, HIDDEN:NODES],
+                rhs=w0_given_codes[:, HIDDEN:NODES].bitcast(FP8X4),
+                rhs_scale=w0_given_plane[:, HIDDEN:NODES],
                 start=True,
                 stop=False,
             )
@@ -218,10 +237,14 @@ def tile_spn_kernel(tc, x, w0_words, w0_scales, w1_words, w1_scales, biases, out
             tiles = slice(rnd * TILES_PER_ROUND, (rnd + 1) * TILES_PER_ROUND)
             nc.sync.dma_start(out=out_by_tile[:, tiles, :], in_=out_sb[:, tiles, :])
 
+        reorder_w0_plane()
+        reorder_w0_codes(0)
         quantise_x(0)
         bias_ps = psum_x.tile([P, P], BF16, tag="xt")
         nc.tensor.transpose(bias_ps[:], bias_rows[:], ident_bf16[:])
         nc.vector.tensor_copy(out=bias_col[:], in_=bias_ps[:, 0 : HIDDEN // P])
+        for g in range(1, GROUPS):
+            reorder_w0_codes(g)
 
         for step in range(UNITS + SECOND_LAG + 1):
             if step < UNITS:

@@ -32,7 +32,7 @@ UNITS = ROUNDS * GROUPS
 
 REGROUP_LAG = 1
 QUANTISE_LAG = 2
-SECOND_LAG = 8
+SECOND_LAG = 5
 
 FLOPS = 2 * TOKENS * INPUTS * NODES + 2 * TOKENS * HIDDEN * OUTPUTS
 
@@ -42,13 +42,12 @@ def tile_spn_kernel(tc, x, w0_words, w0_scales, w1_words, w1_scales, biases, out
     with ExitStack() as stack:
         keep = stack.enter_context(tc.tile_pool(name="keep", bufs=1))
         x_stage = stack.enter_context(tc.tile_pool(name="x_stage", bufs=2))
-        rows_pool = stack.enter_context(tc.tile_pool(name="rows", bufs=8))
-        planes_pool = stack.enter_context(tc.tile_pool(name="planes", bufs=4))
+        rows_pool = stack.enter_context(tc.tile_pool(name="rows", bufs=12))
+        planes_pool = stack.enter_context(tc.tile_pool(name="planes", bufs=5))
         grouped_pool = stack.enter_context(tc.tile_pool(name="grouped", bufs=3))
         hq_pool = stack.enter_context(tc.tile_pool(name="hq", bufs=3))
-        psum_x = stack.enter_context(tc.psum_pool(name="psum_x", bufs=2))
-        psum_z = stack.enter_context(tc.psum_pool(name="psum_z", bufs=4))
-        psum_o = stack.enter_context(tc.psum_pool(name="psum_o", bufs=2))
+        psum_work = stack.enter_context(tc.psum_pool(name="psum_work", bufs=4))
+        psum_acc = stack.enter_context(tc.psum_pool(name="psum_acc", bufs=4))
         stack.enter_context(tc.manual_schedule())
 
         x_sb = keep.tile([P, TOKEN_TILES, INPUTS], BF16)
@@ -111,8 +110,11 @@ def tile_spn_kernel(tc, x, w0_words, w0_scales, w1_words, w1_scales, biases, out
         load_x(2)
         load_x(3)
 
-        def quantise_x(rnd):
+        x_grouped_of = {}
+
+        def transpose_x(rnd):
             x_grouped = x_stage.tile([P, BLOCK, PACK], BF16, align_bytes=64)
+            x_grouped_of[rnd] = x_grouped
             grouped_words = (
                 x_grouped[:]
                 .rearrange("p r t -> p (r t)")
@@ -121,24 +123,26 @@ def tile_spn_kernel(tc, x, w0_words, w0_scales, w1_words, w1_scales, biases, out
             )
             banks = []
             for pair in range(TILES_PER_ROUND // 2):
-                xt = psum_x.tile([P, 2, 2, P], F32, tag="xt")
+                xt = psum_acc.tile([P, 2, 2, P], F32, tag="acc")
                 banks.append(xt)
                 for i in range(2):
                     a = rnd * TILES_PER_ROUND + 2 * pair + i
                     words = x_sb[:, a, :].bitcast(F32).rearrange("p (q u) -> p u q", u=2)
                     for u in range(2):
                         nc.tensor.transpose(xt[:, i, u, :], words[:, u, :], ident_f32[:])
-            nc.scalar.copy(
-                out=grouped_words[:, 0:2, :, :], in_=banks[0][:].rearrange("p i u r -> p i r u")
-            )
-            nc.vector.tensor_copy(
-                out=grouped_words[:, 2:4, :, :], in_=banks[1][:].rearrange("p i u r -> p i r u")
-            )
+            empty_bank = nc.scalar.copy if rnd == 0 else nc.vector.tensor_copy
+            for pair in range(TILES_PER_ROUND // 2):
+                empty_bank(
+                    out=grouped_words[:, 2 * pair : 2 * pair + 2, :, :],
+                    in_=banks[pair][:].rearrange("p i u r -> p i r u"),
+                )
+
+        def quantise_x(rnd):
             cols = slice(rnd * BLOCK, (rnd + 1) * BLOCK)
             nc.vector.quantize_mx(
                 out=xq_codes[:, cols].bitcast(FP8X4),
                 scales=xq_plane[:, cols],
-                in_=x_grouped[:].rearrange("p r t -> p (r t)"),
+                in_=x_grouped_of[rnd][:].rearrange("p r t -> p (r t)"),
             )
 
         def reorder_w0_plane():
@@ -162,29 +166,29 @@ def tile_spn_kernel(tc, x, w0_words, w0_scales, w1_words, w1_scales, biases, out
         grouped_of = {}
         hq_of = {}
 
-        def first_product(unit):
+        def first_product(unit, part):
             rnd, g = divmod(unit, GROUPS)
             cols = slice(rnd * BLOCK, (rnd + 1) * BLOCK)
-            planes = planes_pool.tile([P, PACK, BLOCK], BF16)
-            planes_of[unit] = planes
-            for part in range(NODE_TILES_PER_GROUP):
-                j = g * NODE_TILES_PER_GROUP + part
-                nodes = slice(j * P, (j + 1) * P)
-                z = psum_z.tile([P, BLOCK], F32)
-                nc.tensor.matmul_mx(
-                    out=z[:],
-                    lhsT=w0_codes[:, nodes].bitcast(FP8X4),
-                    lhsT_scale=w0_plane[:, nodes],
-                    rhs=xq_codes[:, cols].bitcast(FP8X4),
-                    rhs_scale=xq_plane[:, cols],
-                    start=True,
-                    stop=True,
-                )
-                h_rows = rows_pool.tile([P, BLOCK], BF16)
-                nc.scalar.activation(
-                    out=h_rows[:], in_=z[:], func=RELU, bias=bias_col[:, j : j + 1], scale=1.0
-                )
-                nc.sync.dma_start(out=planes[part:P:NODE_TILES_PER_GROUP, :, :], in_=h_rows[:])
+            if part == 0:
+                planes = planes_pool.tile([P, PACK, BLOCK], BF16)
+                planes_of[unit] = planes
+            j = g * NODE_TILES_PER_GROUP + part
+            nodes = slice(j * P, (j + 1) * P)
+            z = psum_work.tile([P, BLOCK], F32)
+            nc.tensor.matmul_mx(
+                out=z[:],
+                lhsT=w0_codes[:, nodes].bitcast(FP8X4),
+                lhsT_scale=w0_plane[:, nodes],
+                rhs=xq_codes[:, cols].bitcast(FP8X4),
+                rhs_scale=xq_plane[:, cols],
+                start=True,
+                stop=True,
+            )
+            h_rows = rows_pool.tile([P, BLOCK], BF16)
+            nc.scalar.activation(
+                out=h_rows[:], in_=z[:], func=RELU, bias=bias_col[:, j : j + 1], scale=1.0
+            )
+            nc.sync.dma_start(out=planes_of[unit][part:P:NODE_TILES_PER_GROUP, :, :], in_=h_rows[:])
 
         def regroup(unit):
             grouped = grouped_pool.tile([P, BLOCK, PACK], BF16, align_bytes=64)
@@ -207,31 +211,42 @@ def tile_spn_kernel(tc, x, w0_words, w0_scales, w1_words, w1_scales, biases, out
                 in_=grouped_of[unit][:].rearrange("p r t -> p (r t)"),
             )
 
-        def second_product(a):
+        acc_of = {}
+
+        def h_pass(a, g, stop):
             rnd, i = divmod(a, TILES_PER_ROUND)
             hq_codes, hq_plane = hq_of[rnd]
             tile_cols = slice(i * P, (i + 1) * P)
-            acc = psum_o.tile([P, OUTPUTS], F32)
             nc.tensor.matmul_mx(
-                out=acc[:],
-                lhsT=xq_codes[:, a * P : (a + 1) * P].bitcast(FP8X4),
-                lhsT_scale=xq_plane[:, a * P : (a + 1) * P],
-                rhs=w0_given_codes[:, HIDDEN:NODES].bitcast(FP8X4),
-                rhs_scale=w0_given_plane[:, HIDDEN:NODES],
-                start=True,
-                stop=False,
+                out=acc_of[a][:],
+                lhsT=hq_codes[:, g, tile_cols].bitcast(FP8X4),
+                lhsT_scale=hq_plane[:, g, tile_cols],
+                rhs=w1_codes[:, g, :].bitcast(FP8X4),
+                rhs_scale=w1_plane[:, g, :],
+                start=False,
+                stop=stop,
             )
-            for g in range(GROUPS):
+
+        def second_product(a, g):
+            if g == 1:
+                acc = psum_acc.tile([P, OUTPUTS], F32, tag="acc")
+                acc_of[a] = acc
                 nc.tensor.matmul_mx(
                     out=acc[:],
-                    lhsT=hq_codes[:, g, tile_cols].bitcast(FP8X4),
-                    lhsT_scale=hq_plane[:, g, tile_cols],
-                    rhs=w1_codes[:, g, :].bitcast(FP8X4),
-                    rhs_scale=w1_plane[:, g, :],
-                    start=False,
-                    stop=(g == GROUPS - 1),
+                    lhsT=xq_codes[:, a * P : (a + 1) * P].bitcast(FP8X4),
+                    lhsT_scale=xq_plane[:, a * P : (a + 1) * P],
+                    rhs=w0_given_codes[:, HIDDEN:NODES].bitcast(FP8X4),
+                    rhs_scale=w0_given_plane[:, HIDDEN:NODES],
+                    start=True,
+                    stop=False,
                 )
-            nc.vector.tensor_tensor(out=out_sb[:, a, :], in0=acc[:], in1=bias_out[:], op=ADD)
+                h_pass(a, 0, False)
+            if g >= 1:
+                h_pass(a, g, g == GROUPS - 1)
+            if g == GROUPS - 1:
+                nc.vector.tensor_tensor(
+                    out=out_sb[:, a, :], in0=acc_of[a][:], in1=bias_out[:], op=ADD
+                )
 
         def store(rnd):
             tiles = slice(rnd * TILES_PER_ROUND, (rnd + 1) * TILES_PER_ROUND)
@@ -239,25 +254,28 @@ def tile_spn_kernel(tc, x, w0_words, w0_scales, w1_words, w1_scales, biases, out
 
         reorder_w0_plane()
         reorder_w0_codes(0)
+        transpose_x(0)
         quantise_x(0)
-        bias_ps = psum_x.tile([P, P], BF16, tag="xt")
+        bias_ps = psum_acc.tile([P, P], BF16, tag="acc")
         nc.tensor.transpose(bias_ps[:], bias_rows[:], ident_bf16[:])
         nc.vector.tensor_copy(out=bias_col[:], in_=bias_ps[:, 0 : HIDDEN // P])
         for g in range(1, GROUPS):
             reorder_w0_codes(g)
 
         for step in range(UNITS + SECOND_LAG + 1):
-            if step < UNITS:
-                first_product(step)
+            late_round, late_group = divmod(step - SECOND_LAG, GROUPS)
+            for part in range(NODE_TILES_PER_GROUP):
+                if step < UNITS:
+                    first_product(step, part)
+                if 0 <= late_round < ROUNDS:
+                    second_product(late_round * TILES_PER_ROUND + part, late_group)
+            if 1 <= step < ROUNDS:
+                transpose_x(step)
             if 0 <= step - REGROUP_LAG < UNITS:
                 regroup(step - REGROUP_LAG)
             if 0 <= step - QUANTISE_LAG < UNITS:
                 quantise_h(step - QUANTISE_LAG)
-            next_round = step // GROUPS + 1
-            if step % GROUPS == 1 and next_round < ROUNDS:
-                quantise_x(next_round)
-            if 0 <= step - SECOND_LAG < TOKEN_TILES:
-                second_product(step - SECOND_LAG)
-            stored, last = divmod(step - SECOND_LAG - 1, TILES_PER_ROUND)
-            if stored >= 0 and last == TILES_PER_ROUND - 1:
-                store(stored)
+            if 1 <= step - 1 < ROUNDS:
+                quantise_x(step - 1)
+            if 0 < late_round <= ROUNDS and late_group == 0:
+                store(late_round - 1)

@@ -11,6 +11,7 @@ U8 = mybir.dt.uint8
 FP8X4 = mybir.dt.float8_e4m3fn_x4
 RELU = mybir.ActivationFunctionType.Relu
 ADD = mybir.AluOpType.add
+MAX = mybir.AluOpType.max
 
 P = 128
 PACK = 4
@@ -33,6 +34,7 @@ UNITS = ROUNDS * GROUPS
 REGROUP_LAG = 1
 QUANTISE_LAG = 2
 SECOND_LAG = 5
+VECTOR_HELPS_EVERY = 2
 
 FLOPS = 2 * TOKENS * INPUTS * NODES + 2 * TOKENS * HIDDEN * OUTPUTS
 
@@ -185,9 +187,14 @@ def tile_spn_kernel(tc, x, w0_words, w0_scales, w1_words, w1_scales, biases, out
                 stop=True,
             )
             h_rows = rows_pool.tile([P, BLOCK], BF16)
-            nc.scalar.activation(
-                out=h_rows[:], in_=z[:], func=RELU, bias=bias_col[:, j : j + 1], scale=1.0
-            )
+            if part == NODE_TILES_PER_GROUP - 1 and unit % VECTOR_HELPS_EVERY == 0:
+                nc.vector.tensor_scalar(
+                    out=h_rows[:], in0=z[:], scalar1=bias_col[:, j : j + 1], scalar2=0.0, op0=ADD, op1=MAX
+                )
+            else:
+                nc.scalar.activation(
+                    out=h_rows[:], in_=z[:], func=RELU, bias=bias_col[:, j : j + 1], scale=1.0
+                )
             nc.sync.dma_start(out=planes_of[unit][part:P:NODE_TILES_PER_GROUP, :, :], in_=h_rows[:])
 
         def regroup(unit):

@@ -11,7 +11,6 @@ U8 = mybir.dt.uint8
 FP8X4 = mybir.dt.float8_e4m3fn_x4
 RELU = mybir.ActivationFunctionType.Relu
 ADD = mybir.AluOpType.add
-MAX = mybir.AluOpType.max
 
 P = 128
 PACK = 4
@@ -34,7 +33,6 @@ UNITS = ROUNDS * GROUPS
 REGROUP_LAG = 1
 QUANTISE_LAG = 2
 SECOND_LAG = 5
-VECTOR_HELPS_EVERY = 2
 
 FLOPS = 2 * TOKENS * INPUTS * NODES + 2 * TOKENS * HIDDEN * OUTPUTS
 
@@ -61,7 +59,7 @@ def tile_spn_kernel(tc, x, w0_words, w0_scales, w1_words, w1_scales, biases, out
         w0_plane = keep.tile([P, HIDDEN], U8, align_bytes=64)
         w1_codes = keep.tile([P, GROUPS, OUTPUTS], U32, align_bytes=64)
         w1_plane = keep.tile([P, GROUPS, OUTPUTS], U8, align_bytes=64)
-        bias_rows = keep.tile([P, P], BF16)
+        bias_rows = keep.tile([P, GROUPS, P], BF16)
         bias_col = keep.tile([P, HIDDEN // P], F32)
         bias_out = keep.tile([P, OUTPUTS], BF16)
         ident_f32 = keep.tile([P, P], F32)
@@ -77,28 +75,35 @@ def tile_spn_kernel(tc, x, w0_words, w0_scales, w1_words, w1_scales, biases, out
         x_by_tile = x.rearrange("(p a) k -> p a k", a=TOKEN_TILES)
         out_by_tile = out.rearrange("(p a) o -> p a o", a=TOKEN_TILES)
 
-        def load_x(rnd):
-            tiles = slice(rnd * TILES_PER_ROUND, (rnd + 1) * TILES_PER_ROUND)
-            nc.sync.dma_start(out=x_sb[:, tiles, :], in_=x_by_tile[:, tiles, :])
+        def load_x(rnd, pieces):
+            per_piece = TILES_PER_ROUND // pieces
+            for piece in range(pieces):
+                first = rnd * TILES_PER_ROUND + piece * per_piece
+                tiles = slice(first, first + per_piece)
+                nc.sync.dma_start(out=x_sb[:, tiles, :], in_=x_by_tile[:, tiles, :])
 
-        load_x(0)
-        for g in range(GROUPS):
+        w0_words_i32 = w0_words[0].rearrange("p n t -> p (n t)").bitcast(I32)
+
+        def load_w0_codes(first, last):
             nc.sync.dma_start(
-                out=bias_rows[g * PACK : (g + 1) * PACK, :].rearrange("s (w c) -> s w c", c=PACK),
-                in_=biases[g * K_PASS : (g + 1) * K_PASS].rearrange(
-                    "(w s c) -> s w c", s=NODE_TILES_PER_GROUP, c=PACK
-                ),
+                out=w0_given_codes[:, first:last].bitcast(I32), in_=w0_words_i32[:, first:last]
             )
+
+        load_x(0, 2)
+        load_w0_codes(0, K_PASS)
         for quad in range(4):
             nc.sync.dma_start(
                 out=w0_given_plane[32 * quad : 32 * quad + 4, :].bitcast(I32),
                 in_=w0_scales[0, 4 * quad : 4 * quad + 4, :].bitcast(I32),
             )
-        w0_words_i32 = w0_words[0].rearrange("p n t -> p (n t)").bitcast(I32)
-        for first in range(0, NODES, K_PASS):
-            nodes = slice(first, min(first + K_PASS, NODES))
-            nc.sync.dma_start(out=w0_given_codes[:, nodes].bitcast(I32), in_=w0_words_i32[:, nodes])
-        load_x(1)
+        nc.sync.dma_start(
+            out=bias_rows[0:NODE_TILES_PER_GROUP, :, :].rearrange("s g (w c) -> s (g w) c", c=PACK),
+            in_=biases[0:HIDDEN].rearrange("(q s c) -> s q c", s=NODE_TILES_PER_GROUP, c=PACK),
+        )
+        for g in range(1, GROUPS):
+            load_x(g, 1)
+            load_w0_codes(g * K_PASS, (g + 1) * K_PASS)
+        load_w0_codes(HIDDEN, NODES)
         for quad in range(4):
             nc.sync.dma_start(
                 out=w1_plane[32 * quad : 32 * quad + 4, :, :].bitcast(I32),
@@ -109,8 +114,6 @@ def tile_spn_kernel(tc, x, w0_words, w0_scales, w1_words, w1_scales, biases, out
             in_=w1_words.rearrange("g p n t -> p g (n t)").bitcast(I32),
         )
         nc.sync.dma_start(out=bias_out[:], in_=biases[HIDDEN:NODES].partition_broadcast(P))
-        load_x(2)
-        load_x(3)
 
         x_grouped_of = {}
 
@@ -187,14 +190,9 @@ def tile_spn_kernel(tc, x, w0_words, w0_scales, w1_words, w1_scales, biases, out
                 stop=True,
             )
             h_rows = rows_pool.tile([P, BLOCK], BF16)
-            if part == NODE_TILES_PER_GROUP - 1 and unit % VECTOR_HELPS_EVERY == 0:
-                nc.vector.tensor_scalar(
-                    out=h_rows[:], in0=z[:], scalar1=bias_col[:, j : j + 1], scalar2=0.0, op0=ADD, op1=MAX
-                )
-            else:
-                nc.scalar.activation(
-                    out=h_rows[:], in_=z[:], func=RELU, bias=bias_col[:, j : j + 1], scale=1.0
-                )
+            nc.scalar.activation(
+                out=h_rows[:], in_=z[:], func=RELU, bias=bias_col[:, j : j + 1], scale=1.0
+            )
             nc.sync.dma_start(out=planes_of[unit][part:P:NODE_TILES_PER_GROUP, :, :], in_=h_rows[:])
 
         def regroup(unit):
@@ -256,16 +254,22 @@ def tile_spn_kernel(tc, x, w0_words, w0_scales, w1_words, w1_scales, biases, out
                 )
 
         def store(rnd):
-            tiles = slice(rnd * TILES_PER_ROUND, (rnd + 1) * TILES_PER_ROUND)
-            nc.sync.dma_start(out=out_by_tile[:, tiles, :], in_=out_sb[:, tiles, :])
+            for first in range(rnd * TILES_PER_ROUND, (rnd + 1) * TILES_PER_ROUND, 2):
+                nc.sync.dma_start(
+                    out=out_by_tile[:, first : first + 2, :], in_=out_sb[:, first : first + 2, :]
+                )
 
-        reorder_w0_plane()
         reorder_w0_codes(0)
+        reorder_w0_plane()
         transpose_x(0)
         quantise_x(0)
-        bias_ps = psum_acc.tile([P, P], BF16, tag="acc")
-        nc.tensor.transpose(bias_ps[:], bias_rows[:], ident_bf16[:])
-        nc.vector.tensor_copy(out=bias_col[:], in_=bias_ps[:, 0 : HIDDEN // P])
+        bias_ps = psum_acc.tile([P, GROUPS, P], BF16, tag="acc")
+        for g in range(GROUPS):
+            nc.tensor.transpose(bias_ps[:, g, :], bias_rows[:, g, :], ident_bf16[:])
+        nc.vector.tensor_copy(
+            out=bias_col[:].rearrange("p (g s) -> p g s", g=GROUPS),
+            in_=bias_ps[:, :, 0:NODE_TILES_PER_GROUP],
+        )
         for g in range(1, GROUPS):
             reorder_w0_codes(g)
 
@@ -276,13 +280,13 @@ def tile_spn_kernel(tc, x, w0_words, w0_scales, w1_words, w1_scales, biases, out
                     first_product(step, part)
                 if 0 <= late_round < ROUNDS:
                     second_product(late_round * TILES_PER_ROUND + part, late_group)
-            if 1 <= step < ROUNDS:
-                transpose_x(step)
+            if 1 <= step + 1 < ROUNDS:
+                transpose_x(step + 1)
             if 0 <= step - REGROUP_LAG < UNITS:
                 regroup(step - REGROUP_LAG)
             if 0 <= step - QUANTISE_LAG < UNITS:
                 quantise_h(step - QUANTISE_LAG)
-            if 1 <= step - 1 < ROUNDS:
-                quantise_x(step - 1)
+            if 1 <= step < ROUNDS:
+                quantise_x(step)
             if 0 < late_round <= ROUNDS and late_group == 0:
                 store(late_round - 1)

@@ -42,7 +42,6 @@ def tile_spn_kernel(tc, x, w0_words, w0_scales, w1_words, w1_scales, biases, out
     with ExitStack() as stack:
         keep = stack.enter_context(tc.tile_pool(name="keep", bufs=1))
         x_stage = stack.enter_context(tc.tile_pool(name="x_stage", bufs=2))
-        rows_pool = stack.enter_context(tc.tile_pool(name="rows", bufs=12))
         planes_pool = stack.enter_context(tc.tile_pool(name="planes", bufs=5))
         grouped_pool = stack.enter_context(tc.tile_pool(name="grouped", bufs=3))
         hq_pool = stack.enter_context(tc.tile_pool(name="hq", bufs=3))
@@ -65,6 +64,7 @@ def tile_spn_kernel(tc, x, w0_words, w0_scales, w1_words, w1_scales, biases, out
         ident_f32 = keep.tile([P, P], F32)
         ident_bf16 = keep.tile([P, P], BF16)
         out_sb = keep.tile([P, TOKEN_TILES, OUTPUTS], F32)
+        h_rows_all = keep.tile([P, UNITS * NODE_TILES_PER_GROUP, BLOCK], BF16)
 
         nc.vector.memset(bias_rows[:], 0.0)
         nc.vector.memset(w0_given_plane[:].bitcast(I32), 0)
@@ -189,11 +189,11 @@ def tile_spn_kernel(tc, x, w0_words, w0_scales, w1_words, w1_scales, biases, out
                 start=True,
                 stop=True,
             )
-            h_rows = rows_pool.tile([P, BLOCK], BF16)
+            h_rows = h_rows_all[:, unit * NODE_TILES_PER_GROUP + part, :]
             nc.scalar.activation(
-                out=h_rows[:], in_=z[:], func=RELU, bias=bias_col[:, j : j + 1], scale=1.0
+                out=h_rows, in_=z[:], func=RELU, bias=bias_col[:, j : j + 1], scale=1.0
             )
-            nc.sync.dma_start(out=planes_of[unit][part:P:NODE_TILES_PER_GROUP, :, :], in_=h_rows[:])
+            nc.sync.dma_start(out=planes_of[unit][part:P:NODE_TILES_PER_GROUP, :, :], in_=h_rows)
 
         def regroup(unit):
             grouped = grouped_pool.tile([P, BLOCK, PACK], BF16, align_bytes=64)

@@ -27,12 +27,13 @@ BLOCK = 512
 ROUNDS = TOKENS // BLOCK
 TILES_PER_ROUND = BLOCK // P
 GROUPS = HIDDEN // K_PASS
-NODE_TILES_PER_GROUP = K_PASS // P
-UNITS = ROUNDS * GROUPS
+NODE_TILES = K_PASS // P
+PAIR = 2
+UNITS_PER_ROUND = GROUPS // PAIR
+UNITS = ROUNDS * UNITS_PER_ROUND
 
-REGROUP_LAG = 1
-QUANTISE_LAG = 2
-SECOND_LAG = 5
+QUANTISE_LAG = 1
+SECOND_LAG = 3
 
 FLOPS = 2 * TOKENS * INPUTS * NODES + 2 * TOKENS * HIDDEN * OUTPUTS
 
@@ -42,8 +43,8 @@ def tile_spn_kernel(tc, x, w0_words, w0_scales, w1_words, w1_scales, biases, out
     with ExitStack() as stack:
         keep = stack.enter_context(tc.tile_pool(name="keep", bufs=1))
         x_stage = stack.enter_context(tc.tile_pool(name="x_stage", bufs=2))
-        planes_pool = stack.enter_context(tc.tile_pool(name="planes", bufs=5))
-        grouped_pool = stack.enter_context(tc.tile_pool(name="grouped", bufs=3))
+        planes_pool = stack.enter_context(tc.tile_pool(name="planes", bufs=3))
+        grouped_pool = stack.enter_context(tc.tile_pool(name="grouped", bufs=4))
         hq_pool = stack.enter_context(tc.tile_pool(name="hq", bufs=3))
         psum_work = stack.enter_context(tc.psum_pool(name="psum_work", bufs=4))
         psum_acc = stack.enter_context(tc.psum_pool(name="psum_acc", bufs=4))
@@ -59,12 +60,12 @@ def tile_spn_kernel(tc, x, w0_words, w0_scales, w1_words, w1_scales, biases, out
         w1_codes = keep.tile([P, GROUPS, OUTPUTS], U32, align_bytes=64)
         w1_plane = keep.tile([P, GROUPS, OUTPUTS], U8, align_bytes=64)
         bias_rows = keep.tile([P, GROUPS, P], BF16)
-        bias_col = keep.tile([P, HIDDEN // P], F32)
+        bias_col = keep.tile([P, GROUPS * NODE_TILES], F32)
         bias_out = keep.tile([P, OUTPUTS], BF16)
         ident_f32 = keep.tile([P, P], F32)
         ident_bf16 = keep.tile([P, P], BF16)
         out_sb = keep.tile([P, TOKEN_TILES, OUTPUTS], F32)
-        h_rows_all = keep.tile([P, UNITS * NODE_TILES_PER_GROUP, BLOCK], BF16)
+        h_rows = keep.tile([P, UNITS, NODE_TILES, PAIR, BLOCK], BF16)
 
         nc.vector.memset(bias_rows[:], 0.0)
         nc.vector.memset(w0_given_plane[:].bitcast(I32), 0)
@@ -90,19 +91,20 @@ def tile_spn_kernel(tc, x, w0_words, w0_scales, w1_words, w1_scales, biases, out
             )
 
         load_x(0, 2)
-        load_w0_codes(0, K_PASS)
+        load_w0_codes(0, PAIR * K_PASS)
         for quad in range(4):
             nc.sync.dma_start(
                 out=w0_given_plane[32 * quad : 32 * quad + 4, :].bitcast(I32),
                 in_=w0_scales[0, 4 * quad : 4 * quad + 4, :].bitcast(I32),
             )
         nc.sync.dma_start(
-            out=bias_rows[0:NODE_TILES_PER_GROUP, :, :].rearrange("s g (w c) -> s (g w) c", c=PACK),
-            in_=biases[0:HIDDEN].rearrange("(q s c) -> s q c", s=NODE_TILES_PER_GROUP, c=PACK),
+            out=bias_rows[0:NODE_TILES, :, :].rearrange("s g (w c) -> s (g w) c", c=PACK),
+            in_=biases[0:HIDDEN].rearrange("(q s c) -> s q c", s=NODE_TILES, c=PACK),
         )
-        for g in range(1, GROUPS):
-            load_x(g, 1)
-            load_w0_codes(g * K_PASS, (g + 1) * K_PASS)
+        load_x(1, 1)
+        load_w0_codes(PAIR * K_PASS, HIDDEN)
+        load_x(2, 1)
+        load_x(3, 1)
         load_w0_codes(HIDDEN, NODES)
         for quad in range(4):
             nc.sync.dma_start(
@@ -152,88 +154,85 @@ def tile_spn_kernel(tc, x, w0_words, w0_scales, w1_words, w1_scales, biases, out
 
         def reorder_w0_plane():
             nc.vector.tensor_copy(
-                out=w0_plane[:].bitcast(I32).rearrange("p (g s w) -> p g s w", g=GROUPS, s=4),
+                out=w0_plane[:].bitcast(I32).rearrange("p (g s w) -> p g s w", g=GROUPS, s=NODE_TILES),
                 in_=w0_given_plane[:, 0:HIDDEN]
                 .bitcast(I32)
-                .rearrange("p (g w s) -> p g s w", g=GROUPS, s=4),
+                .rearrange("p (g w s) -> p g s w", g=GROUPS, s=NODE_TILES),
             )
 
         def reorder_w0_codes(g):
             nodes = slice(g * K_PASS, (g + 1) * K_PASS)
             nc.vector.tensor_copy(
-                out=w0_codes[:, nodes].bitcast(I32).rearrange("p (s w c) -> p s w c", s=4, c=PACK),
+                out=w0_codes[:, nodes]
+                .bitcast(I32)
+                .rearrange("p (s w c) -> p s w c", s=NODE_TILES, c=PACK),
                 in_=w0_given_codes[:, nodes]
                 .bitcast(I32)
-                .rearrange("p (w s c) -> p s w c", s=4, c=PACK),
+                .rearrange("p (w s c) -> p s w c", s=NODE_TILES, c=PACK),
             )
 
         planes_of = {}
-        grouped_of = {}
         hq_of = {}
+        acc_of = {}
 
-        def first_product(unit, part):
-            rnd, g = divmod(unit, GROUPS)
+        def first_product(unit, s):
+            rnd, half = divmod(unit, UNITS_PER_ROUND)
             cols = slice(rnd * BLOCK, (rnd + 1) * BLOCK)
-            if part == 0:
-                planes = planes_pool.tile([P, PACK, BLOCK], BF16)
+            if s == 0:
+                planes = planes_pool.tile([P, PACK, PAIR, BLOCK], BF16)
                 planes_of[unit] = planes
-            j = g * NODE_TILES_PER_GROUP + part
-            nodes = slice(j * P, (j + 1) * P)
-            z = psum_work.tile([P, BLOCK], F32)
-            nc.tensor.matmul_mx(
-                out=z[:],
-                lhsT=w0_codes[:, nodes].bitcast(FP8X4),
-                lhsT_scale=w0_plane[:, nodes],
-                rhs=xq_codes[:, cols].bitcast(FP8X4),
-                rhs_scale=xq_plane[:, cols],
-                start=True,
-                stop=True,
-            )
-            h_rows = h_rows_all[:, unit * NODE_TILES_PER_GROUP + part, :]
-            nc.scalar.activation(
-                out=h_rows, in_=z[:], func=RELU, bias=bias_col[:, j : j + 1], scale=1.0
-            )
-            nc.sync.dma_start(out=planes_of[unit][part:P:NODE_TILES_PER_GROUP, :, :], in_=h_rows)
-
-        def regroup(unit):
-            grouped = grouped_pool.tile([P, BLOCK, PACK], BF16, align_bytes=64)
-            grouped_of[unit] = grouped
-            nc.vector.tensor_copy(
-                out=grouped[:].rearrange("p (c i) t -> p c t i", i=4),
-                in_=planes_of[unit][:].rearrange("p t (c i) -> p c t i", i=4),
+            for i in range(PAIR):
+                j = (half * PAIR + i) * NODE_TILES + s
+                nodes = slice(j * P, (j + 1) * P)
+                z = psum_work.tile([P, BLOCK], F32)
+                nc.tensor.matmul_mx(
+                    out=z[:],
+                    lhsT=w0_codes[:, nodes].bitcast(FP8X4),
+                    lhsT_scale=w0_plane[:, nodes],
+                    rhs=xq_codes[:, cols].bitcast(FP8X4),
+                    rhs_scale=xq_plane[:, cols],
+                    start=True,
+                    stop=True,
+                )
+                nc.scalar.activation(
+                    out=h_rows[:, unit, s, i, :],
+                    in_=z[:],
+                    func=RELU,
+                    bias=bias_col[:, j : j + 1],
+                    scale=1.0,
+                )
+            nc.sync.dma_start(
+                out=planes_of[unit][s:P:NODE_TILES, :, :, :], in_=h_rows[:, unit, s, :, :]
             )
 
         def quantise_h(unit):
-            rnd, g = divmod(unit, GROUPS)
-            if g == 0:
+            rnd, half = divmod(unit, UNITS_PER_ROUND)
+            if half == 0:
                 hq_codes = hq_pool.tile([P, GROUPS, BLOCK], U32, align_bytes=64)
                 hq_plane = hq_pool.tile([P, GROUPS, BLOCK], U8, align_bytes=64)
                 hq_of[rnd] = (hq_codes, hq_plane)
             hq_codes, hq_plane = hq_of[rnd]
-            nc.vector.quantize_mx(
-                out=hq_codes[:, g, :].bitcast(FP8X4),
-                scales=hq_plane[:, g, :],
-                in_=grouped_of[unit][:].rearrange("p r t -> p (r t)"),
-            )
+            both = []
+            for i in range(PAIR):
+                grouped = grouped_pool.tile([P, BLOCK, PACK], BF16, align_bytes=64)
+                both.append(grouped)
+                nc.vector.tensor_copy(
+                    out=grouped[:].rearrange("p (c i) t -> p c t i", i=4),
+                    in_=planes_of[unit][:, :, i, :].rearrange("p t (c i) -> p c t i", i=4),
+                )
+            for i in range(PAIR):
+                g = half * PAIR + i
+                nc.vector.quantize_mx(
+                    out=hq_codes[:, g, :].bitcast(FP8X4),
+                    scales=hq_plane[:, g, :],
+                    in_=both[i][:].rearrange("p r t -> p (r t)"),
+                )
 
-        acc_of = {}
-
-        def h_pass(a, g, stop):
-            rnd, i = divmod(a, TILES_PER_ROUND)
+        def second_product(unit, i):
+            rnd, half = divmod(unit, UNITS_PER_ROUND)
             hq_codes, hq_plane = hq_of[rnd]
-            tile_cols = slice(i * P, (i + 1) * P)
-            nc.tensor.matmul_mx(
-                out=acc_of[a][:],
-                lhsT=hq_codes[:, g, tile_cols].bitcast(FP8X4),
-                lhsT_scale=hq_plane[:, g, tile_cols],
-                rhs=w1_codes[:, g, :].bitcast(FP8X4),
-                rhs_scale=w1_plane[:, g, :],
-                start=False,
-                stop=stop,
-            )
-
-        def second_product(a, g):
-            if g == 1:
+            a = rnd * TILES_PER_ROUND + i
+            if half == 0:
                 acc = psum_acc.tile([P, OUTPUTS], F32, tag="acc")
                 acc_of[a] = acc
                 nc.tensor.matmul_mx(
@@ -245,10 +244,17 @@ def tile_spn_kernel(tc, x, w0_words, w0_scales, w1_words, w1_scales, biases, out
                     start=True,
                     stop=False,
                 )
-                h_pass(a, 0, False)
-            if g >= 1:
-                h_pass(a, g, g == GROUPS - 1)
-            if g == GROUPS - 1:
+            for g in range(half * PAIR, (half + 1) * PAIR):
+                nc.tensor.matmul_mx(
+                    out=acc_of[a][:],
+                    lhsT=hq_codes[:, g, i * P : (i + 1) * P].bitcast(FP8X4),
+                    lhsT_scale=hq_plane[:, g, i * P : (i + 1) * P],
+                    rhs=w1_codes[:, g, :].bitcast(FP8X4),
+                    rhs_scale=w1_plane[:, g, :],
+                    start=False,
+                    stop=(g == GROUPS - 1),
+                )
+            if half == UNITS_PER_ROUND - 1:
                 nc.vector.tensor_tensor(
                     out=out_sb[:, a, :], in0=acc_of[a][:], in1=bias_out[:], op=ADD
                 )
@@ -259,7 +265,8 @@ def tile_spn_kernel(tc, x, w0_words, w0_scales, w1_words, w1_scales, biases, out
                     out=out_by_tile[:, first : first + 2, :], in_=out_sb[:, first : first + 2, :]
                 )
 
-        reorder_w0_codes(0)
+        for g in range(PAIR):
+            reorder_w0_codes(g)
         reorder_w0_plane()
         transpose_x(0)
         quantise_x(0)
@@ -268,25 +275,23 @@ def tile_spn_kernel(tc, x, w0_words, w0_scales, w1_words, w1_scales, biases, out
             nc.tensor.transpose(bias_ps[:, g, :], bias_rows[:, g, :], ident_bf16[:])
         nc.vector.tensor_copy(
             out=bias_col[:].rearrange("p (g s) -> p g s", g=GROUPS),
-            in_=bias_ps[:, :, 0:NODE_TILES_PER_GROUP],
+            in_=bias_ps[:, :, 0:NODE_TILES],
         )
-        for g in range(1, GROUPS):
+        for g in range(PAIR, GROUPS):
             reorder_w0_codes(g)
 
         for step in range(UNITS + SECOND_LAG + 1):
-            late_round, late_group = divmod(step - SECOND_LAG, GROUPS)
-            for part in range(NODE_TILES_PER_GROUP):
+            for s in range(NODE_TILES):
                 if step < UNITS:
-                    first_product(step, part)
-                if 0 <= late_round < ROUNDS:
-                    second_product(late_round * TILES_PER_ROUND + part, late_group)
-            if 1 <= step + 1 < ROUNDS:
+                    first_product(step, s)
+                if 0 <= step - SECOND_LAG < UNITS:
+                    second_product(step - SECOND_LAG, s)
+            if step + 1 < ROUNDS:
                 transpose_x(step + 1)
-            if 0 <= step - REGROUP_LAG < UNITS:
-                regroup(step - REGROUP_LAG)
             if 0 <= step - QUANTISE_LAG < UNITS:
                 quantise_h(step - QUANTISE_LAG)
-            if 1 <= step < ROUNDS:
-                quantise_x(step)
-            if 0 < late_round <= ROUNDS and late_group == 0:
-                store(late_round - 1)
+            if step + 1 < ROUNDS:
+                quantise_x(step + 1)
+            stored, first_half = divmod(step - SECOND_LAG, UNITS_PER_ROUND)
+            if 0 < stored <= ROUNDS and first_half == 0:
+                store(stored - 1)

@@ -59,19 +59,15 @@ def tile_spn_kernel(tc, x, w0_words, w0_scales, w1_words, w1_scales, biases, out
         w0_plane = keep.tile([P, HIDDEN], U8, align_bytes=64)
         w1_codes = keep.tile([P, GROUPS, OUTPUTS], U32, align_bytes=64)
         w1_plane = keep.tile([P, GROUPS, OUTPUTS], U8, align_bytes=64)
-        bias_rows = keep.tile([P, GROUPS, P], BF16)
+        bias_given = keep.tile([P, GROUPS * NODE_TILES], BF16)
         bias_col = keep.tile([P, GROUPS * NODE_TILES], F32)
         bias_out = keep.tile([P, OUTPUTS], BF16)
         ident_f32 = keep.tile([P, P], F32)
-        ident_bf16 = keep.tile([P, P], BF16)
         out_sb = keep.tile([P, TOKEN_TILES, OUTPUTS], F32)
-        h_rows = keep.tile([P, UNITS, NODE_TILES, PAIR, BLOCK], BF16)
 
-        nc.vector.memset(bias_rows[:], 0.0)
         nc.vector.memset(w0_given_plane[:].bitcast(I32), 0)
         nc.vector.memset(w1_plane[:].bitcast(I32), 0)
         make_identity(nc, ident_f32[:])
-        make_identity(nc, ident_bf16[:])
 
         x_by_tile = x.rearrange("(p a) k -> p a k", a=TOKEN_TILES)
         out_by_tile = out.rearrange("(p a) o -> p a o", a=TOKEN_TILES)
@@ -98,8 +94,8 @@ def tile_spn_kernel(tc, x, w0_words, w0_scales, w1_words, w1_scales, biases, out
                 in_=w0_scales[0, 4 * quad : 4 * quad + 4, :].bitcast(I32),
             )
         nc.sync.dma_start(
-            out=bias_rows[0:NODE_TILES, :, :].rearrange("s g (w c) -> s (g w) c", c=PACK),
-            in_=biases[0:HIDDEN].rearrange("(q s c) -> s q c", s=NODE_TILES, c=PACK),
+            out=bias_given[:].rearrange("p (g s) -> p g s", g=GROUPS),
+            in_=biases[0:HIDDEN].rearrange("(g p s) -> p g s", g=GROUPS, s=NODE_TILES),
         )
         load_x(1, 1)
         load_w0_codes(PAIR * K_PASS, HIDDEN)
@@ -152,23 +148,15 @@ def tile_spn_kernel(tc, x, w0_words, w0_scales, w1_words, w1_scales, biases, out
                 in_=x_grouped_of[rnd][:].rearrange("p r t -> p (r t)"),
             )
 
-        def reorder_w0_plane():
-            nc.vector.tensor_copy(
-                out=w0_plane[:].bitcast(I32).rearrange("p (g s w) -> p g s w", g=GROUPS, s=NODE_TILES),
-                in_=w0_given_plane[:, 0:HIDDEN]
-                .bitcast(I32)
-                .rearrange("p (g w s) -> p g s w", g=GROUPS, s=NODE_TILES),
-            )
-
-        def reorder_w0_codes(g):
+        def reorder_w0(g):
             nodes = slice(g * K_PASS, (g + 1) * K_PASS)
             nc.vector.tensor_copy(
-                out=w0_codes[:, nodes]
-                .bitcast(I32)
-                .rearrange("p (s w c) -> p s w c", s=NODE_TILES, c=PACK),
-                in_=w0_given_codes[:, nodes]
-                .bitcast(I32)
-                .rearrange("p (w s c) -> p s w c", s=NODE_TILES, c=PACK),
+                out=w0_codes[:, nodes].bitcast(I32).rearrange("p (s m) -> p s m", s=NODE_TILES),
+                in_=w0_given_codes[:, nodes].bitcast(I32).rearrange("p (m s) -> p s m", s=NODE_TILES),
+            )
+            nc.vector.tensor_copy(
+                out=w0_plane[:, nodes].rearrange("p (s m) -> p s m", s=NODE_TILES),
+                in_=w0_given_plane[:, nodes].rearrange("p (m s) -> p s m", s=NODE_TILES),
             )
 
         planes_of = {}
@@ -195,15 +183,12 @@ def tile_spn_kernel(tc, x, w0_words, w0_scales, w1_words, w1_scales, biases, out
                     stop=True,
                 )
                 nc.scalar.activation(
-                    out=h_rows[:, unit, s, i, :],
+                    out=planes_of[unit][:, s, i, :],
                     in_=z[:],
                     func=RELU,
                     bias=bias_col[:, j : j + 1],
                     scale=1.0,
                 )
-            nc.sync.dma_start(
-                out=planes_of[unit][s:P:NODE_TILES, :, :, :], in_=h_rows[:, unit, s, :, :]
-            )
 
         def quantise_h(unit):
             rnd, half = divmod(unit, UNITS_PER_ROUND)
@@ -266,19 +251,12 @@ def tile_spn_kernel(tc, x, w0_words, w0_scales, w1_words, w1_scales, biases, out
                 )
 
         for g in range(PAIR):
-            reorder_w0_codes(g)
-        reorder_w0_plane()
+            reorder_w0(g)
+        nc.vector.tensor_copy(out=bias_col[:], in_=bias_given[:])
         transpose_x(0)
         quantise_x(0)
-        bias_ps = psum_acc.tile([P, GROUPS, P], BF16, tag="acc")
-        for g in range(GROUPS):
-            nc.tensor.transpose(bias_ps[:, g, :], bias_rows[:, g, :], ident_bf16[:])
-        nc.vector.tensor_copy(
-            out=bias_col[:].rearrange("p (g s) -> p g s", g=GROUPS),
-            in_=bias_ps[:, :, 0:NODE_TILES],
-        )
         for g in range(PAIR, GROUPS):
-            reorder_w0_codes(g)
+            reorder_w0(g)
 
         for step in range(UNITS + SECOND_LAG + 1):
             for s in range(NODE_TILES):

@@ -11,6 +11,7 @@ U8 = mybir.dt.uint8
 FP8X4 = mybir.dt.float8_e4m3fn_x4
 RELU = mybir.ActivationFunctionType.Relu
 ADD = mybir.AluOpType.add
+MAX = mybir.AluOpType.max
 
 P = 128
 PACK = 4
@@ -27,13 +28,11 @@ BLOCK = 512
 ROUNDS = TOKENS // BLOCK
 TILES_PER_ROUND = BLOCK // P
 GROUPS = HIDDEN // K_PASS
-NODE_TILES = K_PASS // P
-PAIR = 2
-UNITS_PER_ROUND = GROUPS // PAIR
-UNITS = ROUNDS * UNITS_PER_ROUND
+UNITS = ROUNDS * GROUPS
+BANKS = 8
 
-QUANTISE_LAG = 1
 SECOND_LAG = 3
+TILES_PER_STEP = 2
 
 FLOPS = 2 * TOKENS * INPUTS * NODES + 2 * TOKENS * HIDDEN * OUTPUTS
 
@@ -43,11 +42,9 @@ def tile_spn_kernel(tc, x, w0_words, w0_scales, w1_words, w1_scales, biases, out
     with ExitStack() as stack:
         keep = stack.enter_context(tc.tile_pool(name="keep", bufs=1))
         x_stage = stack.enter_context(tc.tile_pool(name="x_stage", bufs=2))
-        planes_pool = stack.enter_context(tc.tile_pool(name="planes", bufs=3))
-        grouped_pool = stack.enter_context(tc.tile_pool(name="grouped", bufs=4))
-        hq_pool = stack.enter_context(tc.tile_pool(name="hq", bufs=3))
-        psum_work = stack.enter_context(tc.psum_pool(name="psum_work", bufs=4))
-        psum_acc = stack.enter_context(tc.psum_pool(name="psum_acc", bufs=4))
+        planes_pool = stack.enter_context(tc.tile_pool(name="planes", bufs=5))
+        grouped_pool = stack.enter_context(tc.tile_pool(name="grouped", bufs=3))
+        psum = stack.enter_context(tc.psum_pool(name="psum", bufs=BANKS))
         stack.enter_context(tc.manual_schedule())
 
         x_sb = keep.tile([P, TOKEN_TILES, INPUTS], BF16)
@@ -59,8 +56,10 @@ def tile_spn_kernel(tc, x, w0_words, w0_scales, w1_words, w1_scales, biases, out
         w0_plane = keep.tile([P, HIDDEN], U8, align_bytes=64)
         w1_codes = keep.tile([P, GROUPS, OUTPUTS], U32, align_bytes=64)
         w1_plane = keep.tile([P, GROUPS, OUTPUTS], U8, align_bytes=64)
-        bias_given = keep.tile([P, GROUPS * NODE_TILES], BF16)
-        bias_col = keep.tile([P, GROUPS * NODE_TILES], F32)
+        hq_codes = keep.tile([P, UNITS, BLOCK], U32, align_bytes=64)
+        hq_plane = keep.tile([P, UNITS, BLOCK], U8, align_bytes=64)
+        bias_given = keep.tile([P, GROUPS * PACK], BF16)
+        bias_col = keep.tile([P, GROUPS * PACK], F32)
         bias_out = keep.tile([P, OUTPUTS], BF16)
         ident_f32 = keep.tile([P, P], F32)
         out_sb = keep.tile([P, TOKEN_TILES, OUTPUTS], F32)
@@ -87,18 +86,19 @@ def tile_spn_kernel(tc, x, w0_words, w0_scales, w1_words, w1_scales, biases, out
             )
 
         load_x(0, 2)
-        load_w0_codes(0, PAIR * K_PASS)
         for quad in range(4):
             nc.sync.dma_start(
                 out=w0_given_plane[32 * quad : 32 * quad + 4, :].bitcast(I32),
                 in_=w0_scales[0, 4 * quad : 4 * quad + 4, :].bitcast(I32),
             )
+        load_w0_codes(0, K_PASS)
         nc.sync.dma_start(
-            out=bias_given[:].rearrange("p (g s) -> p g s", g=GROUPS),
-            in_=biases[0:HIDDEN].rearrange("(g p s) -> p g s", g=GROUPS, s=NODE_TILES),
+            out=bias_given[:].rearrange("p (g t) -> p g t", g=GROUPS),
+            in_=biases[0:HIDDEN].rearrange("(g p t) -> p g t", g=GROUPS, t=PACK),
         )
+        load_w0_codes(K_PASS, 2 * K_PASS)
         load_x(1, 1)
-        load_w0_codes(PAIR * K_PASS, HIDDEN)
+        load_w0_codes(2 * K_PASS, HIDDEN)
         load_x(2, 1)
         load_x(3, 1)
         load_w0_codes(HIDDEN, NODES)
@@ -114,8 +114,21 @@ def tile_spn_kernel(tc, x, w0_words, w0_scales, w1_words, w1_scales, biases, out
         nc.sync.dma_start(out=bias_out[:], in_=biases[HIDDEN:NODES].partition_broadcast(P))
 
         x_grouped_of = {}
+        x_banks_of = {}
 
         def transpose_x(rnd):
+            banks = []
+            for pair in range(TILES_PER_ROUND // 2):
+                xt = psum.tile([P, 2, 2, P], F32, tag="bank")
+                banks.append(xt)
+                for i in range(2):
+                    a = rnd * TILES_PER_ROUND + 2 * pair + i
+                    words = x_sb[:, a, :].bitcast(F32).rearrange("p (q u) -> p u q", u=2)
+                    for u in range(2):
+                        nc.tensor.transpose(xt[:, i, u, :], words[:, u, :], ident_f32[:])
+            x_banks_of[rnd] = banks
+
+        def empty_x(rnd, engines):
             x_grouped = x_stage.tile([P, BLOCK, PACK], BF16, align_bytes=64)
             x_grouped_of[rnd] = x_grouped
             grouped_words = (
@@ -124,20 +137,10 @@ def tile_spn_kernel(tc, x, w0_words, w0_scales, w1_words, w1_scales, biases, out
                 .bitcast(F32)
                 .rearrange("p (i r u) -> p i r u", i=TILES_PER_ROUND, u=2)
             )
-            banks = []
             for pair in range(TILES_PER_ROUND // 2):
-                xt = psum_acc.tile([P, 2, 2, P], F32, tag="acc")
-                banks.append(xt)
-                for i in range(2):
-                    a = rnd * TILES_PER_ROUND + 2 * pair + i
-                    words = x_sb[:, a, :].bitcast(F32).rearrange("p (q u) -> p u q", u=2)
-                    for u in range(2):
-                        nc.tensor.transpose(xt[:, i, u, :], words[:, u, :], ident_f32[:])
-            empty_bank = nc.scalar.copy if rnd == 0 else nc.vector.tensor_copy
-            for pair in range(TILES_PER_ROUND // 2):
-                empty_bank(
+                engines[pair](
                     out=grouped_words[:, 2 * pair : 2 * pair + 2, :, :],
-                    in_=banks[pair][:].rearrange("p i u r -> p i r u"),
+                    in_=x_banks_of[rnd][pair][:].rearrange("p i u r -> p i r u"),
                 )
 
         def quantise_x(rnd):
@@ -151,77 +154,77 @@ def tile_spn_kernel(tc, x, w0_words, w0_scales, w1_words, w1_scales, biases, out
         def reorder_w0(g):
             nodes = slice(g * K_PASS, (g + 1) * K_PASS)
             nc.vector.tensor_copy(
-                out=w0_codes[:, nodes].bitcast(I32).rearrange("p (s m) -> p s m", s=NODE_TILES),
-                in_=w0_given_codes[:, nodes].bitcast(I32).rearrange("p (m s) -> p s m", s=NODE_TILES),
+                out=w0_plane[:, nodes].rearrange("p (t m) -> p t m", t=PACK),
+                in_=w0_given_plane[:, nodes].rearrange("p (m t) -> p t m", t=PACK),
             )
             nc.vector.tensor_copy(
-                out=w0_plane[:, nodes].rearrange("p (s m) -> p s m", s=NODE_TILES),
-                in_=w0_given_plane[:, nodes].rearrange("p (m s) -> p s m", s=NODE_TILES),
+                out=w0_codes[:, nodes].bitcast(I32).rearrange("p (t m) -> p t m", t=PACK),
+                in_=w0_given_codes[:, nodes].bitcast(I32).rearrange("p (m t) -> p t m", t=PACK),
             )
 
         planes_of = {}
-        hq_of = {}
-        acc_of = {}
+        grouped_of = {}
 
-        def first_product(unit, s):
-            rnd, half = divmod(unit, UNITS_PER_ROUND)
+        def first_product(unit, t, on_vector):
+            rnd, g = divmod(unit, GROUPS)
             cols = slice(rnd * BLOCK, (rnd + 1) * BLOCK)
-            if s == 0:
-                planes = planes_pool.tile([P, PACK, PAIR, BLOCK], BF16)
+            if t == 0:
+                planes = planes_pool.tile([P, PACK, BLOCK], BF16)
                 planes_of[unit] = planes
-            for i in range(PAIR):
-                j = (half * PAIR + i) * NODE_TILES + s
-                nodes = slice(j * P, (j + 1) * P)
-                z = psum_work.tile([P, BLOCK], F32)
-                nc.tensor.matmul_mx(
-                    out=z[:],
-                    lhsT=w0_codes[:, nodes].bitcast(FP8X4),
-                    lhsT_scale=w0_plane[:, nodes],
-                    rhs=xq_codes[:, cols].bitcast(FP8X4),
-                    rhs_scale=xq_plane[:, cols],
-                    start=True,
-                    stop=True,
+            j = g * PACK + t
+            nodes = slice(j * P, (j + 1) * P)
+            z = psum.tile([P, BLOCK], F32, tag="bank")
+            nc.tensor.matmul_mx(
+                out=z[:],
+                lhsT=w0_codes[:, nodes].bitcast(FP8X4),
+                lhsT_scale=w0_plane[:, nodes],
+                rhs=xq_codes[:, cols].bitcast(FP8X4),
+                rhs_scale=xq_plane[:, cols],
+                start=True,
+                stop=True,
+            )
+            if on_vector:
+                nc.vector.tensor_scalar(
+                    out=planes_of[unit][:, t, :],
+                    in0=z[:],
+                    scalar1=bias_col[:, j : j + 1],
+                    scalar2=0.0,
+                    op0=ADD,
+                    op1=MAX,
                 )
+            else:
                 nc.scalar.activation(
-                    out=planes_of[unit][:, s, i, :],
+                    out=planes_of[unit][:, t, :],
                     in_=z[:],
                     func=RELU,
                     bias=bias_col[:, j : j + 1],
                     scale=1.0,
                 )
 
-        def quantise_h(unit):
-            rnd, half = divmod(unit, UNITS_PER_ROUND)
-            if half == 0:
-                hq_codes = hq_pool.tile([P, GROUPS, BLOCK], U32, align_bytes=64)
-                hq_plane = hq_pool.tile([P, GROUPS, BLOCK], U8, align_bytes=64)
-                hq_of[rnd] = (hq_codes, hq_plane)
-            hq_codes, hq_plane = hq_of[rnd]
-            both = []
-            for i in range(PAIR):
-                grouped = grouped_pool.tile([P, BLOCK, PACK], BF16, align_bytes=64)
-                both.append(grouped)
-                nc.vector.tensor_copy(
-                    out=grouped[:].rearrange("p (c i) t -> p c t i", i=4),
-                    in_=planes_of[unit][:, :, i, :].rearrange("p t (c i) -> p c t i", i=4),
-                )
-            for i in range(PAIR):
-                g = half * PAIR + i
-                nc.vector.quantize_mx(
-                    out=hq_codes[:, g, :].bitcast(FP8X4),
-                    scales=hq_plane[:, g, :],
-                    in_=both[i][:].rearrange("p r t -> p (r t)"),
-                )
+        def interleave(unit, first=0, count=BLOCK, copy=nc.vector.tensor_copy):
+            grouped = grouped_pool.tile([P, count, PACK], BF16, align_bytes=64, tag="grouped")
+            grouped_of[(unit, first)] = grouped
+            copy(
+                out=grouped[:].rearrange("p (c i) t -> p c t i", i=4),
+                in_=planes_of[unit][:, :, first : first + count].rearrange("p t (c i) -> p c t i", i=4),
+            )
 
-        def second_product(unit, i):
-            rnd, half = divmod(unit, UNITS_PER_ROUND)
-            hq_codes, hq_plane = hq_of[rnd]
-            a = rnd * TILES_PER_ROUND + i
-            if half == 0:
-                acc = psum_acc.tile([P, OUTPUTS], F32, tag="acc")
+        def quantise_h(unit, first=0, count=BLOCK):
+            nc.vector.quantize_mx(
+                out=hq_codes[:, unit, first : first + count].bitcast(FP8X4),
+                scales=hq_plane[:, unit, first : first + count],
+                in_=grouped_of[(unit, first)][:].rearrange("p r t -> p (r t)"),
+            )
+
+        acc_of = {}
+
+        def second_product(a, groups):
+            rnd, i = divmod(a, TILES_PER_ROUND)
+            if groups[0] == 0:
+                acc = psum.tile([P, BLOCK], F32, tag="bank")
                 acc_of[a] = acc
                 nc.tensor.matmul_mx(
-                    out=acc[:],
+                    out=acc[:, 0:OUTPUTS],
                     lhsT=xq_codes[:, a * P : (a + 1) * P].bitcast(FP8X4),
                     lhsT_scale=xq_plane[:, a * P : (a + 1) * P],
                     rhs=w0_given_codes[:, HIDDEN:NODES].bitcast(FP8X4),
@@ -229,47 +232,75 @@ def tile_spn_kernel(tc, x, w0_words, w0_scales, w1_words, w1_scales, biases, out
                     start=True,
                     stop=False,
                 )
-            for g in range(half * PAIR, (half + 1) * PAIR):
+            for g in groups:
+                unit = rnd * GROUPS + g
                 nc.tensor.matmul_mx(
-                    out=acc_of[a][:],
-                    lhsT=hq_codes[:, g, i * P : (i + 1) * P].bitcast(FP8X4),
-                    lhsT_scale=hq_plane[:, g, i * P : (i + 1) * P],
+                    out=acc_of[a][:, 0:OUTPUTS],
+                    lhsT=hq_codes[:, unit, i * P : (i + 1) * P].bitcast(FP8X4),
+                    lhsT_scale=hq_plane[:, unit, i * P : (i + 1) * P],
                     rhs=w1_codes[:, g, :].bitcast(FP8X4),
                     rhs_scale=w1_plane[:, g, :],
                     start=False,
                     stop=(g == GROUPS - 1),
                 )
-            if half == UNITS_PER_ROUND - 1:
-                nc.vector.tensor_tensor(
-                    out=out_sb[:, a, :], in0=acc_of[a][:], in1=bias_out[:], op=ADD
-                )
 
-        def store(rnd):
-            for first in range(rnd * TILES_PER_ROUND, (rnd + 1) * TILES_PER_ROUND, 2):
-                nc.sync.dma_start(
-                    out=out_by_tile[:, first : first + 2, :], in_=out_sb[:, first : first + 2, :]
-                )
+        def finish(a):
+            nc.vector.tensor_tensor(
+                out=out_sb[:, a, :], in0=acc_of[a][:, 0:OUTPUTS], in1=bias_out[:], op=ADD
+            )
 
-        for g in range(PAIR):
-            reorder_w0(g)
-        nc.vector.tensor_copy(out=bias_col[:], in_=bias_given[:])
+        def store(first, count):
+            nc.sync.dma_start(
+                out=out_by_tile[:, first : first + count, :], in_=out_sb[:, first : first + count, :]
+            )
+
+        reorder_w0(0)
         transpose_x(0)
+        empty_x(0, (nc.scalar.copy, nc.scalar.copy))
         quantise_x(0)
-        for g in range(PAIR, GROUPS):
-            reorder_w0(g)
+        nc.vector.tensor_copy(out=bias_col[:], in_=bias_given[:])
+        reorder_w0(1)
 
-        for step in range(UNITS + SECOND_LAG + 1):
-            for s in range(NODE_TILES):
-                if step < UNITS:
-                    first_product(step, s)
-                if 0 <= step - SECOND_LAG < UNITS:
-                    second_product(step - SECOND_LAG, s)
+        early_tiles = TOKEN_TILES - TILES_PER_ROUND
+        for step in range(UNITS):
+            for t in range(PACK):
+                first_product(step, t, on_vector=(step == 0 and t % 2 == 1))
             if step + 1 < ROUNDS:
                 transpose_x(step + 1)
-            if 0 <= step - QUANTISE_LAG < UNITS:
-                quantise_h(step - QUANTISE_LAG)
+            rnd, late = divmod(step - (GROUPS - 1) - SECOND_LAG, GROUPS)
+            tiles = []
+            if rnd >= 0 and late * TILES_PER_STEP < TILES_PER_ROUND:
+                first = rnd * TILES_PER_ROUND + late * TILES_PER_STEP
+                tiles = [a for a in range(first, first + TILES_PER_STEP) if a < early_tiles]
+            for a in tiles:
+                second_product(a, list(range(GROUPS)))
+            for a in tiles:
+                finish(a)
+            if tiles:
+                store(tiles[0], len(tiles))
+            if step + 2 < GROUPS:
+                reorder_w0(step + 2)
+            if step + 1 < ROUNDS:
+                empty_x(step + 1, (nc.scalar.copy, nc.scalar.copy))
+            if step < UNITS - 1:
+                interleave(step)
             if step + 1 < ROUNDS:
                 quantise_x(step + 1)
-            stored, first_half = divmod(step - SECOND_LAG, UNITS_PER_ROUND)
-            if 0 < stored <= ROUNDS and first_half == 0:
-                store(stored - 1)
+            if step > 0:
+                quantise_h(step - 1)
+
+        half = BLOCK // 2
+        interleave(UNITS - 1, 0, half)
+        interleave(UNITS - 1, half, half, nc.scalar.copy)
+        last = list(range(early_tiles, TOKEN_TILES))
+        for g in range(GROUPS - 1):
+            for a in last:
+                second_product(a, [g])
+        quantise_h(UNITS - 1, 0, half)
+        quantise_h(UNITS - 1, half, half)
+        for a in last:
+            second_product(a, [GROUPS - 1])
+        for a in last:
+            finish(a)
+            if a % 2 == 1:
+                store(a - 1, 2)

@@ -143,12 +143,13 @@ def tile_spn_kernel(tc, x, w0_words, w0_scales, w1_words, w1_scales, biases, out
                     in_=x_banks_of[rnd][pair][:].rearrange("p i u r -> p i r u"),
                 )
 
-        def quantise_x(rnd):
-            cols = slice(rnd * BLOCK, (rnd + 1) * BLOCK)
+        def quantise_x(rnd, part=0, parts=1):
+            count = BLOCK // parts
+            cols = slice(rnd * BLOCK + part * count, rnd * BLOCK + (part + 1) * count)
             nc.vector.quantize_mx(
                 out=xq_codes[:, cols].bitcast(FP8X4),
                 scales=xq_plane[:, cols],
-                in_=x_grouped_of[rnd][:].rearrange("p r t -> p (r t)"),
+                in_=x_grouped_of[rnd][:, part * count : (part + 1) * count, :].rearrange("p r t -> p (r t)"),
             )
 
         def reorder_w0(g):
@@ -165,17 +166,19 @@ def tile_spn_kernel(tc, x, w0_words, w0_scales, w1_words, w1_scales, biases, out
         planes_of = {}
         grouped_of = {}
 
-        def first_product(unit, t, on_vector):
+        def first_product(unit, t, on_vector, part=0, parts=1):
             rnd, g = divmod(unit, GROUPS)
-            cols = slice(rnd * BLOCK, (rnd + 1) * BLOCK)
-            if t == 0:
+            count = BLOCK // parts
+            mine = slice(part * count, (part + 1) * count)
+            cols = slice(rnd * BLOCK + mine.start, rnd * BLOCK + mine.stop)
+            if t == 0 and part == 0:
                 planes = planes_pool.tile([P, PACK, BLOCK], BF16)
                 planes_of[unit] = planes
             j = g * PACK + t
             nodes = slice(j * P, (j + 1) * P)
             z = psum.tile([P, BLOCK], F32, tag="bank")
             nc.tensor.matmul_mx(
-                out=z[:],
+                out=z[:, 0:count],
                 lhsT=w0_codes[:, nodes].bitcast(FP8X4),
                 lhsT_scale=w0_plane[:, nodes],
                 rhs=xq_codes[:, cols].bitcast(FP8X4),
@@ -185,8 +188,8 @@ def tile_spn_kernel(tc, x, w0_words, w0_scales, w1_words, w1_scales, biases, out
             )
             if on_vector:
                 nc.vector.tensor_scalar(
-                    out=planes_of[unit][:, t, :],
-                    in0=z[:],
+                    out=planes_of[unit][:, t, mine],
+                    in0=z[:, 0:count],
                     scalar1=bias_col[:, j : j + 1],
                     scalar2=0.0,
                     op0=ADD,
@@ -194,10 +197,10 @@ def tile_spn_kernel(tc, x, w0_words, w0_scales, w1_words, w1_scales, biases, out
                 )
             else:
                 nc.scalar.activation(
-                    out=planes_of[unit][:, t, :],
-                    in_=z[:],
+                    out=planes_of[unit][:, t, mine],
+                    in_=z[:, 0:count],
                     func=RELU,
-                    bias=bias_col[:, j : j + 1],
+                    bias=bias_given[:, j : j + 1],
                     scale=1.0,
                 )
 
@@ -257,16 +260,20 @@ def tile_spn_kernel(tc, x, w0_words, w0_scales, w1_words, w1_scales, biases, out
         reorder_w0(0)
         transpose_x(0)
         empty_x(0, (nc.scalar.copy, nc.scalar.copy))
-        quantise_x(0)
+        quantise_x(0, 0, 2)
+        quantise_x(0, 1, 2)
         nc.vector.tensor_copy(out=bias_col[:], in_=bias_given[:])
         reorder_w0(1)
 
         early_tiles = TOKEN_TILES - TILES_PER_ROUND
         for step in range(UNITS):
-            for t in range(PACK):
-                first_product(step, t, on_vector=(step == 0 and t % 2 == 1))
-            if step + 1 < ROUNDS:
-                transpose_x(step + 1)
+            parts = 2 if step == 0 else 1
+            for part in range(parts):
+                for t in range(PACK):
+                    first_product(step, t, step == 0 and t % 2 == 1, part, parts)
+            nxt = step // GROUPS + 1 if step % GROUPS == 1 and step // GROUPS + 1 < ROUNDS else 0
+            if nxt:
+                transpose_x(nxt)
             rnd, late = divmod(step - (GROUPS - 1) - SECOND_LAG, GROUPS)
             tiles = []
             if rnd >= 0 and late * TILES_PER_STEP < TILES_PER_ROUND:
@@ -280,12 +287,12 @@ def tile_spn_kernel(tc, x, w0_words, w0_scales, w1_words, w1_scales, biases, out
                 store(tiles[0], len(tiles))
             if step + 2 < GROUPS:
                 reorder_w0(step + 2)
-            if step + 1 < ROUNDS:
-                empty_x(step + 1, (nc.scalar.copy, nc.scalar.copy))
+            if nxt:
+                empty_x(nxt, (nc.scalar.copy, nc.vector.tensor_copy))
             if step < UNITS - 1:
                 interleave(step)
-            if step + 1 < ROUNDS:
-                quantise_x(step + 1)
+            if nxt:
+                quantise_x(nxt)
             if step > 0:
                 quantise_h(step - 1)
 

@@ -281,10 +281,11 @@ def tile_spn_kernel(tc, x, w0_words, w0_scales, w1_words, w1_scales, biases, out
                 tiles = [a for a in range(first, first + TILES_PER_STEP) if a < early_tiles]
             for a in tiles:
                 second_product(a, list(range(GROUPS)))
-            for a in tiles:
-                finish(a)
-            if tiles:
-                store(tiles[0], len(tiles))
+            if step < UNITS - 1:
+                for a in tiles:
+                    finish(a)
+                if tiles:
+                    store(tiles[0], len(tiles))
             if step + 2 < GROUPS:
                 reorder_w0(step + 2)
             if nxt:
@@ -299,6 +300,9 @@ def tile_spn_kernel(tc, x, w0_words, w0_scales, w1_words, w1_scales, biases, out
         half = BLOCK // 2
         interleave(UNITS - 1, 0, half)
         interleave(UNITS - 1, half, half, nc.scalar.copy)
+        for a in tiles:
+            finish(a)
+        store(tiles[0], len(tiles))
         last = list(range(early_tiles, TOKEN_TILES))
         for g in range(GROUPS - 1):
             for a in last:
@@ -309,5 +313,4 @@ def tile_spn_kernel(tc, x, w0_words, w0_scales, w1_words, w1_scales, biases, out
             second_product(a, [GROUPS - 1])
         for a in last:
             finish(a)
-            if a % 2 == 1:
-                store(a - 1, 2)
+            store(a, 1)

@@ -85,17 +85,21 @@ def tile_spn_kernel(tc, x, w0_words, w0_scales, w1_words, w1_scales, biases, out
                 out=w0_given_codes[:, first:last].bitcast(I32), in_=w0_words_i32[:, first:last]
             )
 
+        def load_w0_scales(first, last):
+            for quad in range(4):
+                nc.sync.dma_start(
+                    out=w0_given_plane[32 * quad : 32 * quad + 4, first:last].bitcast(I32),
+                    in_=w0_scales[0, 4 * quad : 4 * quad + 4, first:last].bitcast(I32),
+                )
+
         load_x(0, 2)
-        for quad in range(4):
-            nc.sync.dma_start(
-                out=w0_given_plane[32 * quad : 32 * quad + 4, :].bitcast(I32),
-                in_=w0_scales[0, 4 * quad : 4 * quad + 4, :].bitcast(I32),
-            )
+        load_w0_scales(0, K_PASS)
         load_w0_codes(0, K_PASS)
         nc.sync.dma_start(
             out=bias_given[:].rearrange("p (g t) -> p g t", g=GROUPS),
             in_=biases[0:HIDDEN].rearrange("(g p t) -> p g t", g=GROUPS, t=PACK),
         )
+        load_w0_scales(K_PASS, NODES)
         load_w0_codes(K_PASS, 2 * K_PASS)
         load_x(1, 1)
         load_w0_codes(2 * K_PASS, HIDDEN)

@@ -51,11 +51,12 @@ def tile_spn_kernel(tc, x, w0_words, w0_scales, w1_words, w1_scales, biases, out
         xq_codes = keep.tile([P, TOKENS], U32, align_bytes=64)
         xq_plane = keep.tile([P, TOKENS], U8, align_bytes=64)
         w0_given_codes = keep.tile([P, NODES], U32, align_bytes=64)
-        w0_given_plane = keep.tile([P, NODES], U8, align_bytes=64)
+        w0_given_plane = keep.tile([P, K_PASS], U8, align_bytes=64)
+        w0_out_plane = keep.tile([P, OUTPUTS], U8, align_bytes=64)
         w0_codes = keep.tile([P, HIDDEN], U32, align_bytes=64)
-        w0_plane = keep.tile([P, HIDDEN], U8, align_bytes=64)
+        w0_plane = keep.tile([P, K_PASS], U8, align_bytes=64)
         w1_codes = keep.tile([P, GROUPS, OUTPUTS], U32, align_bytes=64)
-        w1_plane = keep.tile([P, GROUPS, OUTPUTS], U8, align_bytes=64)
+        w1_plane = keep.tile([P, OUTPUTS], U8, align_bytes=64)
         hq_codes = keep.tile([P, UNITS, BLOCK], U32, align_bytes=64)
         hq_plane = keep.tile([P, UNITS, BLOCK], U8, align_bytes=64)
         bias_given = keep.tile([P, GROUPS * PACK], BF16)
@@ -65,6 +66,7 @@ def tile_spn_kernel(tc, x, w0_words, w0_scales, w1_words, w1_scales, biases, out
         out_sb = keep.tile([P, TOKEN_TILES, OUTPUTS], F32)
 
         nc.vector.memset(w0_given_plane[:].bitcast(I32), 0)
+        nc.vector.memset(w0_out_plane[:].bitcast(I32), 0)
         nc.vector.memset(w1_plane[:].bitcast(I32), 0)
         make_identity(nc, ident_f32[:])
 
@@ -85,21 +87,20 @@ def tile_spn_kernel(tc, x, w0_words, w0_scales, w1_words, w1_scales, biases, out
                 out=w0_given_codes[:, first:last].bitcast(I32), in_=w0_words_i32[:, first:last]
             )
 
-        def load_w0_scales(first, last):
+        def load_packed_scales(plane, given):
             for quad in range(4):
                 nc.sync.dma_start(
-                    out=w0_given_plane[32 * quad : 32 * quad + 4, first:last].bitcast(I32),
-                    in_=w0_scales[0, 4 * quad : 4 * quad + 4, first:last].bitcast(I32),
+                    out=plane[32 * quad : 32 * quad + 4 * GROUPS, :].bitcast(I32),
+                    in_=given[:, 4 * quad : 4 * quad + 4, :].bitcast(I32),
                 )
 
         load_x(0, 2)
-        load_w0_scales(0, K_PASS)
+        load_packed_scales(w0_given_plane, w0_scales[0, :, 0:HIDDEN].rearrange("q (g n) -> g q n", g=GROUPS))
         load_w0_codes(0, K_PASS)
         nc.sync.dma_start(
             out=bias_given[:].rearrange("p (g t) -> p g t", g=GROUPS),
             in_=biases[0:HIDDEN].rearrange("(g p t) -> p g t", g=GROUPS, t=PACK),
         )
-        load_w0_scales(K_PASS, NODES)
         load_w0_codes(K_PASS, 2 * K_PASS)
         load_x(1, 1)
         load_w0_codes(2 * K_PASS, HIDDEN)
@@ -108,9 +109,10 @@ def tile_spn_kernel(tc, x, w0_words, w0_scales, w1_words, w1_scales, biases, out
         load_w0_codes(HIDDEN, NODES)
         for quad in range(4):
             nc.sync.dma_start(
-                out=w1_plane[32 * quad : 32 * quad + 4, :, :].bitcast(I32),
-                in_=w1_scales[:, 4 * quad : 4 * quad + 4, :].rearrange("g r n -> r g n").bitcast(I32),
+                out=w0_out_plane[32 * quad : 32 * quad + 4, :].bitcast(I32),
+                in_=w0_scales[0, 4 * quad : 4 * quad + 4, HIDDEN:NODES].bitcast(I32),
             )
+        load_packed_scales(w1_plane, w1_scales)
         nc.sync.dma_start(
             out=w1_codes[:].bitcast(I32),
             in_=w1_words.rearrange("g p n t -> p g (n t)").bitcast(I32),
@@ -158,10 +160,11 @@ def tile_spn_kernel(tc, x, w0_words, w0_scales, w1_words, w1_scales, biases, out
 
         def reorder_w0(g):
             nodes = slice(g * K_PASS, (g + 1) * K_PASS)
-            nc.vector.tensor_copy(
-                out=w0_plane[:, nodes].rearrange("p (t m) -> p t m", t=PACK),
-                in_=w0_given_plane[:, nodes].rearrange("p (m t) -> p t m", t=PACK),
-            )
+            if g == 0:
+                nc.vector.tensor_copy(
+                    out=w0_plane[:].rearrange("p (t m) -> p t m", t=PACK),
+                    in_=w0_given_plane[:].rearrange("p (m t) -> p t m", t=PACK),
+                )
             nc.vector.tensor_copy(
                 out=w0_codes[:, nodes].bitcast(I32).rearrange("p (t m) -> p t m", t=PACK),
                 in_=w0_given_codes[:, nodes].bitcast(I32).rearrange("p (m t) -> p t m", t=PACK),
@@ -184,7 +187,7 @@ def tile_spn_kernel(tc, x, w0_words, w0_scales, w1_words, w1_scales, biases, out
             nc.tensor.matmul_mx(
                 out=z[:, 0:count],
                 lhsT=w0_codes[:, nodes].bitcast(FP8X4),
-                lhsT_scale=w0_plane[:, nodes],
+                lhsT_scale=w0_plane[4 * g : P, t * P : (t + 1) * P],
                 rhs=xq_codes[:, cols].bitcast(FP8X4),
                 rhs_scale=xq_plane[:, cols],
                 start=True,
@@ -235,7 +238,7 @@ def tile_spn_kernel(tc, x, w0_words, w0_scales, w1_words, w1_scales, biases, out
                     lhsT=xq_codes[:, a * P : (a + 1) * P].bitcast(FP8X4),
                     lhsT_scale=xq_plane[:, a * P : (a + 1) * P],
                     rhs=w0_given_codes[:, HIDDEN:NODES].bitcast(FP8X4),
-                    rhs_scale=w0_given_plane[:, HIDDEN:NODES],
+                    rhs_scale=w0_out_plane[:],
                     start=True,
                     stop=False,
                 )
@@ -246,7 +249,7 @@ def tile_spn_kernel(tc, x, w0_words, w0_scales, w1_words, w1_scales, biases, out
                     lhsT=hq_codes[:, unit, i * P : (i + 1) * P].bitcast(FP8X4),
                     lhsT_scale=hq_plane[:, unit, i * P : (i + 1) * P],
                     rhs=w1_codes[:, g, :].bitcast(FP8X4),
-                    rhs_scale=w1_plane[:, g, :],
+                    rhs_scale=w1_plane[4 * g : P, :],
                     start=False,
                     stop=(g == GROUPS - 1),
                 )

@@ -70,6 +70,14 @@ def tile_spn_kernel(tc, x, w0_words, w0_scales, w1_words, w1_scales, biases, out
         nc.vector.memset(w1_plane[:].bitcast(I32), 0)
         make_identity(nc, ident_f32[:])
 
+        zeros = keep.tile([P, BLOCK], BF16)
+        nc.vector.memset(zeros[:], 0.0)
+
+        def warm(count):
+            idle = psum.tile([P, BLOCK], F32, tag="bank")
+            for i in range(count):
+                nc.tensor.matmul(idle[:], lhsT=zeros[:, 0:P], rhs=zeros[:], start=True, stop=True)
+
         x_by_tile = x.rearrange("(p a) k -> p a k", a=TOKEN_TILES)
         out_by_tile = out.rearrange("(p a) o -> p a o", a=TOKEN_TILES)
 
@@ -265,7 +273,9 @@ def tile_spn_kernel(tc, x, w0_words, w0_scales, w1_words, w1_scales, biases, out
             )
 
         reorder_w0(0)
+        warm(5)
         transpose_x(0)
+        warm(2)
         empty_x(0, (nc.scalar.copy, nc.scalar.copy))
         quantise_x(0, 0, 2)
         quantise_x(0, 1, 2)

@@ -43,7 +43,7 @@ def tile_spn_kernel(tc, x, w0_words, w0_scales, w1_words, w1_scales, biases, out
         keep = stack.enter_context(tc.tile_pool(name="keep", bufs=1))
         x_stage = stack.enter_context(tc.tile_pool(name="x_stage", bufs=2))
         planes_pool = stack.enter_context(tc.tile_pool(name="planes", bufs=5))
-        grouped_pool = stack.enter_context(tc.tile_pool(name="grouped", bufs=3))
+        grouped_pool = stack.enter_context(tc.tile_pool(name="grouped", bufs=6))
         psum = stack.enter_context(tc.psum_pool(name="psum", bufs=BANKS))
         stack.enter_context(tc.manual_schedule())
 
@@ -71,7 +71,7 @@ def tile_spn_kernel(tc, x, w0_words, w0_scales, w1_words, w1_scales, biases, out
         make_identity(nc, ident_f32[:])
 
         zeros = keep.tile([P, BLOCK], BF16)
-        nc.vector.memset(zeros[:], 0.0)
+        nc.vector.memset(zeros[:].bitcast(I32), 0)
 
         def warm(count):
             idle = psum.tile([P, BLOCK], F32, tag="bank")
@@ -105,11 +105,11 @@ def tile_spn_kernel(tc, x, w0_words, w0_scales, w1_words, w1_scales, biases, out
         load_x(0, 2)
         load_packed_scales(w0_given_plane, w0_scales[0, :, 0:HIDDEN].rearrange("q (g n) -> g q n", g=GROUPS))
         load_w0_codes(0, K_PASS)
+        load_w0_codes(K_PASS, 2 * K_PASS)
         nc.sync.dma_start(
             out=bias_given[:].rearrange("p (g t) -> p g t", g=GROUPS),
             in_=biases[0:HIDDEN].rearrange("(g p t) -> p g t", g=GROUPS, t=PACK),
         )
-        load_w0_codes(K_PASS, 2 * K_PASS)
         load_x(1, 1)
         load_w0_codes(2 * K_PASS, HIDDEN)
         load_x(2, 1)
@@ -128,52 +128,47 @@ def tile_spn_kernel(tc, x, w0_words, w0_scales, w1_words, w1_scales, biases, out
         nc.sync.dma_start(out=bias_out[:], in_=biases[HIDDEN:NODES].partition_broadcast(P))
 
         x_grouped_of = {}
-        x_banks_of = {}
+        x_bank_of = {}
 
-        def transpose_x(rnd):
-            banks = []
-            for pair in range(TILES_PER_ROUND // 2):
-                xt = psum.tile([P, 2, 2, P], F32, tag="bank")
-                banks.append(xt)
-                for i in range(2):
-                    a = rnd * TILES_PER_ROUND + 2 * pair + i
-                    words = x_sb[:, a, :].bitcast(F32).rearrange("p (q u) -> p u q", u=2)
-                    for u in range(2):
-                        nc.tensor.transpose(xt[:, i, u, :], words[:, u, :], ident_f32[:])
-            x_banks_of[rnd] = banks
+        def transpose_x(a, count):
+            xt = psum.tile([P, 2, 2, P], F32, tag="bank")
+            for i in range(count):
+                words = x_sb[:, a + i, :].bitcast(F32).rearrange("p (q u) -> p u q", u=2)
+                for u in range(2):
+                    nc.tensor.transpose(xt[:, i, u, :], words[:, u, :], ident_f32[:])
+            x_bank_of[a] = xt
 
-        def empty_x(rnd, engines):
-            x_grouped = x_stage.tile([P, BLOCK, PACK], BF16, align_bytes=64)
-            x_grouped_of[rnd] = x_grouped
-            grouped_words = (
-                x_grouped[:]
+        def empty_x(a, count, copy):
+            rnd, i = divmod(a, TILES_PER_ROUND)
+            if i == 0:
+                x_grouped = x_stage.tile([P, BLOCK, PACK], BF16, align_bytes=64)
+                x_grouped_of[rnd] = x_grouped
+            words = (
+                x_grouped_of[rnd][:, i * P : (i + count) * P, :]
                 .rearrange("p r t -> p (r t)")
                 .bitcast(F32)
-                .rearrange("p (i r u) -> p i r u", i=TILES_PER_ROUND, u=2)
+                .rearrange("p (i r u) -> p i r u", i=count, u=2)
             )
-            for pair in range(TILES_PER_ROUND // 2):
-                engines[pair](
-                    out=grouped_words[:, 2 * pair : 2 * pair + 2, :, :],
-                    in_=x_banks_of[rnd][pair][:].rearrange("p i u r -> p i r u"),
-                )
+            copy(out=words, in_=x_bank_of[a][:, 0:count, :, :].rearrange("p i u r -> p i r u"))
 
-        def quantise_x(rnd, part=0, parts=1):
-            count = BLOCK // parts
-            cols = slice(rnd * BLOCK + part * count, rnd * BLOCK + (part + 1) * count)
+        def quantise_x(a, count):
+            rnd, i = divmod(a, TILES_PER_ROUND)
+            cols = slice(a * P, (a + count) * P)
             nc.vector.quantize_mx(
                 out=xq_codes[:, cols].bitcast(FP8X4),
                 scales=xq_plane[:, cols],
-                in_=x_grouped_of[rnd][:, part * count : (part + 1) * count, :].rearrange("p r t -> p (r t)"),
+                in_=x_grouped_of[rnd][:, i * P : (i + count) * P, :].rearrange("p r t -> p (r t)"),
             )
 
-        def reorder_w0(g):
-            nodes = slice(g * K_PASS, (g + 1) * K_PASS)
-            if g == 0:
-                nc.vector.tensor_copy(
-                    out=w0_plane[:].rearrange("p (t m) -> p t m", t=PACK),
-                    in_=w0_given_plane[:].rearrange("p (m t) -> p t m", t=PACK),
-                )
+        def reorder_scales():
             nc.vector.tensor_copy(
+                out=w0_plane[:].rearrange("p (t m) -> p t m", t=PACK),
+                in_=w0_given_plane[:].rearrange("p (m t) -> p t m", t=PACK),
+            )
+
+        def reorder_w0(g, copy=nc.vector.tensor_copy):
+            nodes = slice(g * K_PASS, (g + 1) * K_PASS)
+            copy(
                 out=w0_codes[:, nodes].bitcast(I32).rearrange("p (t m) -> p t m", t=PACK),
                 in_=w0_given_codes[:, nodes].bitcast(I32).rearrange("p (m t) -> p t m", t=PACK),
             )
@@ -181,26 +176,50 @@ def tile_spn_kernel(tc, x, w0_words, w0_scales, w1_words, w1_scales, biases, out
         planes_of = {}
         grouped_of = {}
 
-        def first_product(unit, t, on_vector, part=0, parts=1):
+        def first_pass(z, unit, t, first, count):
             rnd, g = divmod(unit, GROUPS)
-            count = BLOCK // parts
-            mine = slice(part * count, (part + 1) * count)
-            cols = slice(rnd * BLOCK + mine.start, rnd * BLOCK + mine.stop)
-            if t == 0 and part == 0:
-                planes = planes_pool.tile([P, PACK, BLOCK], BF16)
-                planes_of[unit] = planes
             j = g * PACK + t
-            nodes = slice(j * P, (j + 1) * P)
-            z = psum.tile([P, BLOCK], F32, tag="bank")
+            cols = slice(rnd * BLOCK + first, rnd * BLOCK + first + count)
             nc.tensor.matmul_mx(
-                out=z[:, 0:count],
-                lhsT=w0_codes[:, nodes].bitcast(FP8X4),
+                out=z,
+                lhsT=w0_codes[:, j * P : (j + 1) * P].bitcast(FP8X4),
                 lhsT_scale=w0_plane[4 * g : P, t * P : (t + 1) * P],
                 rhs=xq_codes[:, cols].bitcast(FP8X4),
                 rhs_scale=xq_plane[:, cols],
                 start=True,
                 stop=True,
             )
+
+        def first_product_grouped(unit, first, count):
+            g = unit % GROUPS
+            grouped = grouped_pool.tile([P, count, PACK], BF16, align_bytes=64, tag="grouped")
+            grouped_of[(unit, first)] = grouped
+            for i in range(count // P):
+                z = psum.tile([P, PACK, P], F32, tag="bank")
+                for t in range(PACK):
+                    first_pass(z[:, t, :], unit, t, first + i * P, P)
+                nc.vector.tensor_tensor(
+                    out=grouped[:, i * P : (i + 1) * P, :],
+                    in0=z[:].rearrange("p t r -> p r t"),
+                    in1=bias_col[:, g * PACK : (g + 1) * PACK].unsqueeze(1).to_broadcast([P, P, PACK]),
+                    op=ADD,
+                )
+
+        def relu(unit, first):
+            values = grouped_of[(unit, first)][:].rearrange("p r t -> p (r t)")
+            nc.vector.tensor_scalar_max(out=values, in0=values, scalar1=0.0)
+
+
+        def first_product(unit, t, on_vector, part=0, parts=1):
+            rnd, g = divmod(unit, GROUPS)
+            count = BLOCK // parts
+            mine = slice(part * count, (part + 1) * count)
+            if t == 0 and part == 0:
+                planes = planes_pool.tile([P, PACK, BLOCK], BF16)
+                planes_of[unit] = planes
+            j = g * PACK + t
+            z = psum.tile([P, BLOCK], F32, tag="bank")
+            first_pass(z[:, 0:count], unit, t, mine.start, count)
             if on_vector:
                 nc.vector.tensor_scalar(
                     out=planes_of[unit][:, t, mine],
@@ -218,6 +237,23 @@ def tile_spn_kernel(tc, x, w0_words, w0_scales, w1_words, w1_scales, biases, out
                     bias=bias_given[:, j : j + 1],
                     scale=1.0,
                 )
+
+        def first_product_part(unit, t, first, count):
+            if unit not in planes_of:
+                planes = planes_pool.tile([P, PACK, BLOCK], BF16)
+                planes_of[unit] = planes
+            j = (unit % GROUPS) * PACK + t
+            z = psum.tile([P, BLOCK], F32, tag="bank")
+            for at in range(0, count, 2 * P):
+                n = min(2 * P, count - at)
+                first_pass(z[:, at : at + n], unit, t, first + at, n)
+            nc.scalar.activation(
+                out=planes_of[unit][:, t, first : first + count],
+                in_=z[:, 0:count],
+                func=RELU,
+                bias=bias_given[:, j : j + 1],
+                scale=1.0,
+            )
 
         def interleave(unit, first=0, count=BLOCK, copy=nc.vector.tensor_copy):
             grouped = grouped_pool.tile([P, count, PACK], BF16, align_bytes=64, tag="grouped")
@@ -272,25 +308,35 @@ def tile_spn_kernel(tc, x, w0_words, w0_scales, w1_words, w1_scales, biases, out
                 out=out_by_tile[:, first : first + count, :], in_=out_sb[:, first : first + count, :]
             )
 
-        reorder_w0(0)
         warm(5)
-        transpose_x(0)
+        for a in range(TILES_PER_ROUND):
+            transpose_x(a, 1)
         warm(2)
-        empty_x(0, (nc.scalar.copy, nc.scalar.copy))
-        quantise_x(0, 0, 2)
-        quantise_x(0, 1, 2)
+        for a in range(TILES_PER_ROUND):
+            empty_x(a, 1, nc.scalar.copy)
+        reorder_scales()
+        quantise_x(0, 1)
+        reorder_w0(0)
+        quantise_x(1, 1)
+        quantise_x(2, 2)
         nc.vector.tensor_copy(out=bias_col[:], in_=bias_given[:])
         reorder_w0(1)
-
         early_tiles = TOKEN_TILES - TILES_PER_ROUND
+        half = BLOCK // 2
         for step in range(UNITS):
             parts = 2 if step == 0 else 1
-            for part in range(parts):
+            if step == UNITS - 1:
                 for t in range(PACK):
-                    first_product(step, t, step == 0 and t % 2 == 1, part, parts)
+                    first_product(step, t, False)
+            else:
+                for part in range(parts):
+                    for t in range(PACK):
+                        first_product(step, t, (step == 0 and t % 2 == 1) or (t == 3 and step == 3), part, parts)
             nxt = step // GROUPS + 1 if step % GROUPS == 1 and step // GROUPS + 1 < ROUNDS else 0
+            x_first = nxt * TILES_PER_ROUND
             if nxt:
-                transpose_x(nxt)
+                transpose_x(x_first, 2)
+                transpose_x(x_first + 2, 2)
             rnd, late = divmod(step - (GROUPS - 1) - SECOND_LAG, GROUPS)
             tiles = []
             if rnd >= 0 and late * TILES_PER_STEP < TILES_PER_ROUND:
@@ -303,30 +349,34 @@ def tile_spn_kernel(tc, x, w0_words, w0_scales, w1_words, w1_scales, biases, out
                     finish(a)
                 if tiles:
                     store(tiles[0], len(tiles))
+            if nxt:
+                empty_x(x_first, 2, nc.scalar.copy)
+                empty_x(x_first + 2, 2, nc.vector.tensor_copy)
+            if step < UNITS - 1:
+                interleave(step)
             if step + 2 < GROUPS:
                 reorder_w0(step + 2)
             if nxt:
-                empty_x(nxt, (nc.scalar.copy, nc.vector.tensor_copy))
-            if step < UNITS - 1:
-                interleave(step)
-            if nxt:
-                quantise_x(nxt)
+                quantise_x(x_first, TILES_PER_ROUND)
             if step > 0:
                 quantise_h(step - 1)
 
-        half = BLOCK // 2
-        interleave(UNITS - 1, 0, half)
-        interleave(UNITS - 1, half, half, nc.scalar.copy)
+        last = list(range(early_tiles, TOKEN_TILES))
+        u = UNITS - 1
+        for i in range(1):
+            interleave(u, i * P, P)
+        for i in range(1, TILES_PER_ROUND):
+            interleave(u, i * P, P, nc.scalar.copy)
         for a in tiles:
             finish(a)
-        store(tiles[0], len(tiles))
-        last = list(range(early_tiles, TOKEN_TILES))
+        if tiles:
+            store(tiles[0], len(tiles))
         for g in range(GROUPS - 1):
             for a in last:
                 second_product(a, [g])
-        quantise_h(UNITS - 1, 0, half)
-        quantise_h(UNITS - 1, half, half)
-        for a in last:
+        for i, a in enumerate(last):
+            quantise_h(u, i * P, P)
+        for i, a in enumerate(last):
             second_product(a, [GROUPS - 1])
         for a in last:
             finish(a)

@@ -105,11 +105,11 @@ def tile_spn_kernel(tc, x, w0_words, w0_scales, w1_words, w1_scales, biases, out
         load_x(0, 2)
         load_packed_scales(w0_given_plane, w0_scales[0, :, 0:HIDDEN].rearrange("q (g n) -> g q n", g=GROUPS))
         load_w0_codes(0, K_PASS)
-        load_w0_codes(K_PASS, 2 * K_PASS)
         nc.sync.dma_start(
             out=bias_given[:].rearrange("p (g t) -> p g t", g=GROUPS),
             in_=biases[0:HIDDEN].rearrange("(g p t) -> p g t", g=GROUPS, t=PACK),
         )
+        load_w0_codes(K_PASS, 2 * K_PASS)
         load_x(1, 1)
         load_w0_codes(2 * K_PASS, HIDDEN)
         load_x(2, 1)
@@ -328,10 +328,14 @@ def tile_spn_kernel(tc, x, w0_words, w0_scales, w1_words, w1_scales, biases, out
             if step == UNITS - 1:
                 for t in range(PACK):
                     first_product(step, t, False)
+            elif step in (3,):
+                for t in range(PACK):
+                    first_product(step, t, False, 0, 2)
+                first_product_grouped(step, half, half)
             else:
                 for part in range(parts):
                     for t in range(PACK):
-                        first_product(step, t, (step == 0 and t % 2 == 1) or (t == 3 and step == 3), part, parts)
+                        first_product(step, t, (step == 0 and t % 2 == 1), part, parts)
             nxt = step // GROUPS + 1 if step % GROUPS == 1 and step // GROUPS + 1 < ROUNDS else 0
             x_first = nxt * TILES_PER_ROUND
             if nxt:
@@ -352,13 +356,19 @@ def tile_spn_kernel(tc, x, w0_words, w0_scales, w1_words, w1_scales, biases, out
             if nxt:
                 empty_x(x_first, 2, nc.scalar.copy)
                 empty_x(x_first + 2, 2, nc.vector.tensor_copy)
-            if step < UNITS - 1:
+            if step in (3,):
+                relu(step, half)
+                interleave(step, 0, half)
+            elif step < UNITS - 1:
                 interleave(step)
             if step + 2 < GROUPS:
                 reorder_w0(step + 2)
             if nxt:
                 quantise_x(x_first, TILES_PER_ROUND)
-            if step > 0:
+            if step - 1 in (3,):
+                quantise_h(step - 1, half, half)
+                quantise_h(step - 1, 0, half)
+            elif step > 0:
                 quantise_h(step - 1)
 
         last = list(range(early_tiles, TOKEN_TILES))

@@ -323,7 +323,7 @@ def tile_spn_kernel(tc, x, w0_words, w0_scales, w1_words, w1_scales, biases, out
         reorder_w0(1)
         early_tiles = TOKEN_TILES - TILES_PER_ROUND
         half = BLOCK // 2
-        for step in range(UNITS):
+        def first_products(step):
             parts = 2 if step == 0 else 1
             if step == UNITS - 1:
                 for t in range(PACK):
@@ -331,11 +331,18 @@ def tile_spn_kernel(tc, x, w0_words, w0_scales, w1_words, w1_scales, biases, out
             elif step in (3,):
                 for t in range(PACK):
                     first_product(step, t, False, 0, 2)
-                first_product_grouped(step, half, half)
             else:
                 for part in range(parts):
                     for t in range(PACK):
                         first_product(step, t, (step == 0 and t % 2 == 1), part, parts)
+
+        issued = []
+        for step in range(UNITS):
+            if step not in issued:
+                first_products(step)
+                issued.append(step)
+            if step + 1 in (3,):
+                first_product_grouped(step + 1, half, half)
             nxt = step // GROUPS + 1 if step % GROUPS == 1 and step // GROUPS + 1 < ROUNDS else 0
             x_first = nxt * TILES_PER_ROUND
             if nxt:
@@ -346,6 +353,9 @@ def tile_spn_kernel(tc, x, w0_words, w0_scales, w1_words, w1_scales, biases, out
             if rnd >= 0 and late * TILES_PER_STEP < TILES_PER_ROUND:
                 first = rnd * TILES_PER_ROUND + late * TILES_PER_STEP
                 tiles = [a for a in range(first, first + TILES_PER_STEP) if a < early_tiles]
+            if (step == UNITS - 2) and step + 1 < UNITS:
+                first_products(step + 1)
+                issued.append(step + 1)
             for a in tiles:
                 second_product(a, list(range(GROUPS)))
             if step < UNITS - 1:
@@ -361,8 +371,9 @@ def tile_spn_kernel(tc, x, w0_words, w0_scales, w1_words, w1_scales, biases, out
                 interleave(step, 0, half)
             elif step < UNITS - 1:
                 interleave(step)
-            if step + 2 < GROUPS:
-                reorder_w0(step + 2)
+            if step == 0:
+                reorder_w0(2)
+                reorder_w0(3)
             if nxt:
                 quantise_x(x_first, TILES_PER_ROUND)
             if step - 1 in (3,):
@@ -373,14 +384,14 @@ def tile_spn_kernel(tc, x, w0_words, w0_scales, w1_words, w1_scales, biases, out
 
         last = list(range(early_tiles, TOKEN_TILES))
         u = UNITS - 1
-        for i in range(1):
-            interleave(u, i * P, P)
-        for i in range(1, TILES_PER_ROUND):
-            interleave(u, i * P, P, nc.scalar.copy)
         for a in tiles:
             finish(a)
         if tiles:
             store(tiles[0], len(tiles))
+        for i in range(1):
+            interleave(u, i * P, P)
+        for i in range(1, TILES_PER_ROUND):
+            interleave(u, i * P, P, nc.scalar.copy)
         for g in range(GROUPS - 1):
             for a in last:
                 second_product(a, [g])

@@ -308,7 +308,7 @@ def tile_spn_kernel(tc, x, w0_words, w0_scales, w1_words, w1_scales, biases, out
                 out=out_by_tile[:, first : first + count, :], in_=out_sb[:, first : first + count, :]
             )
 
-        warm(5)
+        warm(4)
         for a in range(TILES_PER_ROUND):
             transpose_x(a, 1)
         warm(2)

from contextlib import ExitStack

import concourse.mybir as mybir
from concourse.masks import make_identity

F32 = mybir.dt.float32
BF16 = mybir.dt.bfloat16
I32 = mybir.dt.int32
U32 = mybir.dt.uint32
U8 = mybir.dt.uint8
FP8X4 = mybir.dt.float8_e4m3fn_x4
RELU = mybir.ActivationFunctionType.Relu
ADD = mybir.AluOpType.add
MAX = mybir.AluOpType.max

P = 128
PACK = 4
K_PASS = P * PACK

TOKENS = 2048
INPUTS = 512
HIDDEN = 2048
OUTPUTS = 256
NODES = HIDDEN + OUTPUTS

TOKEN_TILES = TOKENS // P
BLOCK = 512
ROUNDS = TOKENS // BLOCK
TILES_PER_ROUND = BLOCK // P
GROUPS = HIDDEN // K_PASS
UNITS = ROUNDS * GROUPS
BANKS = 8

SECOND_LAG = 3
TILES_PER_STEP = 2

FLOPS = 2 * TOKENS * INPUTS * NODES + 2 * TOKENS * HIDDEN * OUTPUTS


def tile_spn_kernel(tc, x, w0_words, w0_scales, w1_words, w1_scales, biases, out):
    nc = tc.nc
    with ExitStack() as stack:
        keep = stack.enter_context(tc.tile_pool(name="keep", bufs=1))
        x_stage = stack.enter_context(tc.tile_pool(name="x_stage", bufs=2))
        planes_pool = stack.enter_context(tc.tile_pool(name="planes", bufs=5))
        grouped_pool = stack.enter_context(tc.tile_pool(name="grouped", bufs=6))
        psum = stack.enter_context(tc.psum_pool(name="psum", bufs=BANKS))
        stack.enter_context(tc.manual_schedule())

        x_sb = keep.tile([P, TOKEN_TILES, INPUTS], BF16)
        xq_codes = keep.tile([P, TOKENS], U32, align_bytes=64)
        xq_plane = keep.tile([P, TOKENS], U8, align_bytes=64)
        w0_given_codes = keep.tile([P, NODES], U32, align_bytes=64)
        w0_given_plane = keep.tile([P, K_PASS], U8, align_bytes=64)
        w0_out_plane = keep.tile([P, OUTPUTS], U8, align_bytes=64)
        w0_codes = keep.tile([P, HIDDEN], U32, align_bytes=64)
        w0_plane = keep.tile([P, K_PASS], U8, align_bytes=64)
        w1_codes = keep.tile([P, GROUPS, OUTPUTS], U32, align_bytes=64)
        w1_plane = keep.tile([P, OUTPUTS], U8, align_bytes=64)
        hq_codes = keep.tile([P, UNITS, BLOCK], U32, align_bytes=64)
        hq_plane = keep.tile([P, UNITS, BLOCK], U8, align_bytes=64)
        bias_given = keep.tile([P, GROUPS * PACK], BF16)
        bias_col = keep.tile([P, GROUPS * PACK], F32)
        bias_out = keep.tile([P, OUTPUTS], BF16)
        ident_f32 = keep.tile([P, P], F32)
        out_sb = keep.tile([P, TOKEN_TILES, OUTPUTS], F32)

        nc.vector.memset(w0_given_plane[:].bitcast(I32), 0)
        nc.vector.memset(w0_out_plane[:].bitcast(I32), 0)
        nc.vector.memset(w1_plane[:].bitcast(I32), 0)
        make_identity(nc, ident_f32[:])

        zeros = keep.tile([P, BLOCK], BF16)
        nc.vector.memset(zeros[:].bitcast(I32), 0)

        def warm(count):
            idle = psum.tile([P, BLOCK], F32, tag="bank")
            for i in range(count):
                nc.tensor.matmul(idle[:], lhsT=zeros[:, 0:P], rhs=zeros[:], start=True, stop=True)

        x_by_tile = x.rearrange("(p a) k -> p a k", a=TOKEN_TILES)
        out_by_tile = out.rearrange("(p a) o -> p a o", a=TOKEN_TILES)

        def load_x(rnd, pieces):
            per_piece = TILES_PER_ROUND // pieces
            for piece in range(pieces):
                first = rnd * TILES_PER_ROUND + piece * per_piece
                tiles = slice(first, first + per_piece)
                nc.sync.dma_start(out=x_sb[:, tiles, :], in_=x_by_tile[:, tiles, :])

        w0_words_i32 = w0_words[0].rearrange("p n t -> p (n t)").bitcast(I32)

        def load_w0_codes(first, last):
            nc.sync.dma_start(
                out=w0_given_codes[:, first:last].bitcast(I32), in_=w0_words_i32[:, first:last]
            )

        def load_packed_scales(plane, given):
            for quad in range(4):
                nc.sync.dma_start(
                    out=plane[32 * quad : 32 * quad + 4 * GROUPS, :].bitcast(I32),
                    in_=given[:, 4 * quad : 4 * quad + 4, :].bitcast(I32),
                )

        load_x(0, 2)
        load_packed_scales(w0_given_plane, w0_scales[0, :, 0:HIDDEN].rearrange("q (g n) -> g q n", g=GROUPS))
        load_w0_codes(0, K_PASS)
        nc.sync.dma_start(
            out=bias_given[:].rearrange("p (g t) -> p g t", g=GROUPS),
            in_=biases[0:HIDDEN].rearrange("(g p t) -> p g t", g=GROUPS, t=PACK),
        )
        load_w0_codes(K_PASS, 2 * K_PASS)
        load_x(1, 1)
        load_w0_codes(2 * K_PASS, HIDDEN)
        load_x(2, 1)
        load_x(3, 1)
        load_w0_codes(HIDDEN, NODES)
        for quad in range(4):
            nc.sync.dma_start(
                out=w0_out_plane[32 * quad : 32 * quad + 4, :].bitcast(I32),
                in_=w0_scales[0, 4 * quad : 4 * quad + 4, HIDDEN:NODES].bitcast(I32),
            )
        load_packed_scales(w1_plane, w1_scales)
        nc.sync.dma_start(
            out=w1_codes[:].bitcast(I32),
            in_=w1_words.rearrange("g p n t -> p g (n t)").bitcast(I32),
        )
        nc.sync.dma_start(out=bias_out[:], in_=biases[HIDDEN:NODES].partition_broadcast(P))

        x_grouped_of = {}
        x_bank_of = {}

        def transpose_x(a, count):
            xt = psum.tile([P, 2, 2, P], F32, tag="bank")
            for i in range(count):
                words = x_sb[:, a + i, :].bitcast(F32).rearrange("p (q u) -> p u q", u=2)
                for u in range(2):
                    nc.tensor.transpose(xt[:, i, u, :], words[:, u, :], ident_f32[:])
            x_bank_of[a] = xt

        def empty_x(a, count, copy):
            rnd, i = divmod(a, TILES_PER_ROUND)
            if i == 0:
                x_grouped = x_stage.tile([P, BLOCK, PACK], BF16, align_bytes=64)
                x_grouped_of[rnd] = x_grouped
            words = (
                x_grouped_of[rnd][:, i * P : (i + count) * P, :]
                .rearrange("p r t -> p (r t)")
                .bitcast(F32)
                .rearrange("p (i r u) -> p i r u", i=count, u=2)
            )
            copy(out=words, in_=x_bank_of[a][:, 0:count, :, :].rearrange("p i u r -> p i r u"))

        def quantise_x(a, count):
            rnd, i = divmod(a, TILES_PER_ROUND)
            cols = slice(a * P, (a + count) * P)
            nc.vector.quantize_mx(
                out=xq_codes[:, cols].bitcast(FP8X4),
                scales=xq_plane[:, cols],
                in_=x_grouped_of[rnd][:, i * P : (i + count) * P, :].rearrange("p r t -> p (r t)"),
            )

        def reorder_scales():
            nc.vector.tensor_copy(
                out=w0_plane[:].rearrange("p (t m) -> p t m", t=PACK),
                in_=w0_given_plane[:].rearrange("p (m t) -> p t m", t=PACK),
            )

        def reorder_w0(g, copy=nc.vector.tensor_copy):
            nodes = slice(g * K_PASS, (g + 1) * K_PASS)
            copy(
                out=w0_codes[:, nodes].bitcast(I32).rearrange("p (t m) -> p t m", t=PACK),
                in_=w0_given_codes[:, nodes].bitcast(I32).rearrange("p (m t) -> p t m", t=PACK),
            )

        planes_of = {}
        grouped_of = {}

        def first_pass(z, unit, t, first, count):
            rnd, g = divmod(unit, GROUPS)
            j = g * PACK + t
            cols = slice(rnd * BLOCK + first, rnd * BLOCK + first + count)
            nc.tensor.matmul_mx(
                out=z,
                lhsT=w0_codes[:, j * P : (j + 1) * P].bitcast(FP8X4),
                lhsT_scale=w0_plane[4 * g : P, t * P : (t + 1) * P],
                rhs=xq_codes[:, cols].bitcast(FP8X4),
                rhs_scale=xq_plane[:, cols],
                start=True,
                stop=True,
            )

        def first_product_grouped(unit, first, count):
            g = unit % GROUPS
            grouped = grouped_pool.tile([P, count, PACK], BF16, align_bytes=64, tag="grouped")
            grouped_of[(unit, first)] = grouped
            for i in range(count // P):
                z = psum.tile([P, PACK, P], F32, tag="bank")
                for t in range(PACK):
                    first_pass(z[:, t, :], unit, t, first + i * P, P)
                nc.vector.tensor_tensor(
                    out=grouped[:, i * P : (i + 1) * P, :],
                    in0=z[:].rearrange("p t r -> p r t"),
                    in1=bias_col[:, g * PACK : (g + 1) * PACK].unsqueeze(1).to_broadcast([P, P, PACK]),
                    op=ADD,
                )

        def relu(unit, first):
            values = grouped_of[(unit, first)][:].rearrange("p r t -> p (r t)")
            nc.vector.tensor_scalar_max(out=values, in0=values, scalar1=0.0)


        def first_product(unit, t, on_vector, part=0, parts=1):
            rnd, g = divmod(unit, GROUPS)
            count = BLOCK // parts
            mine = slice(part * count, (part + 1) * count)
            if t == 0 and part == 0:
                planes = planes_pool.tile([P, PACK, BLOCK], BF16)
                planes_of[unit] = planes
            j = g * PACK + t
            z = psum.tile([P, BLOCK], F32, tag="bank")
            first_pass(z[:, 0:count], unit, t, mine.start, count)
            if on_vector:
                nc.vector.tensor_scalar(
                    out=planes_of[unit][:, t, mine],
                    in0=z[:, 0:count],
                    scalar1=bias_col[:, j : j + 1],
                    scalar2=0.0,
                    op0=ADD,
                    op1=MAX,
                )
            else:
                nc.scalar.activation(
                    out=planes_of[unit][:, t, mine],
                    in_=z[:, 0:count],
                    func=RELU,
                    bias=bias_given[:, j : j + 1],
                    scale=1.0,
                )

        def first_product_part(unit, t, first, count):
            if unit not in planes_of:
                planes = planes_pool.tile([P, PACK, BLOCK], BF16)
                planes_of[unit] = planes
            j = (unit % GROUPS) * PACK + t
            z = psum.tile([P, BLOCK], F32, tag="bank")
            for at in range(0, count, 2 * P):
                n = min(2 * P, count - at)
                first_pass(z[:, at : at + n], unit, t, first + at, n)
            nc.scalar.activation(
                out=planes_of[unit][:, t, first : first + count],
                in_=z[:, 0:count],
                func=RELU,
                bias=bias_given[:, j : j + 1],
                scale=1.0,
            )

        def interleave(unit, first=0, count=BLOCK, copy=nc.vector.tensor_copy):
            grouped = grouped_pool.tile([P, count, PACK], BF16, align_bytes=64, tag="grouped")
            grouped_of[(unit, first)] = grouped
            copy(
                out=grouped[:].rearrange("p (c i) t -> p c t i", i=4),
                in_=planes_of[unit][:, :, first : first + count].rearrange("p t (c i) -> p c t i", i=4),
            )

        def quantise_h(unit, first=0, count=BLOCK):
            nc.vector.quantize_mx(
                out=hq_codes[:, unit, first : first + count].bitcast(FP8X4),
                scales=hq_plane[:, unit, first : first + count],
                in_=grouped_of[(unit, first)][:].rearrange("p r t -> p (r t)"),
            )

        acc_of = {}

        def second_product(a, groups):
            rnd, i = divmod(a, TILES_PER_ROUND)
            if groups[0] == 0:
                acc = psum.tile([P, BLOCK], F32, tag="bank")
                acc_of[a] = acc
                nc.tensor.matmul_mx(
                    out=acc[:, 0:OUTPUTS],
                    lhsT=xq_codes[:, a * P : (a + 1) * P].bitcast(FP8X4),
                    lhsT_scale=xq_plane[:, a * P : (a + 1) * P],
                    rhs=w0_given_codes[:, HIDDEN:NODES].bitcast(FP8X4),
                    rhs_scale=w0_out_plane[:],
                    start=True,
                    stop=False,
                )
            for g in groups:
                unit = rnd * GROUPS + g
                nc.tensor.matmul_mx(
                    out=acc_of[a][:, 0:OUTPUTS],
                    lhsT=hq_codes[:, unit, i * P : (i + 1) * P].bitcast(FP8X4),
                    lhsT_scale=hq_plane[:, unit, i * P : (i + 1) * P],
                    rhs=w1_codes[:, g, :].bitcast(FP8X4),
                    rhs_scale=w1_plane[4 * g : P, :],
                    start=False,
                    stop=(g == GROUPS - 1),
                )

        def finish(a):
            nc.vector.tensor_tensor(
                out=out_sb[:, a, :], in0=acc_of[a][:, 0:OUTPUTS], in1=bias_out[:], op=ADD
            )

        def store(first, count):
            nc.sync.dma_start(
                out=out_by_tile[:, first : first + count, :], in_=out_sb[:, first : first + count, :]
            )

        warm(4)
        for a in range(TILES_PER_ROUND):
            transpose_x(a, 1)
        warm(2)
        for a in range(TILES_PER_ROUND):
            empty_x(a, 1, nc.scalar.copy)
        reorder_scales()
        quantise_x(0, 1)
        reorder_w0(0)
        quantise_x(1, 1)
        quantise_x(2, 2)
        nc.vector.tensor_copy(out=bias_col[:], in_=bias_given[:])
        reorder_w0(1)
        early_tiles = TOKEN_TILES - TILES_PER_ROUND
        half = BLOCK // 2
        def first_products(step):
            parts = 2 if step == 0 else 1
            if step == UNITS - 1:
                for t in range(PACK):
                    first_product(step, t, False)
            elif step in (3,):
                for t in range(PACK):
                    first_product(step, t, False, 0, 2)
            else:
                for part in range(parts):
                    for t in range(PACK):
                        first_product(step, t, (step == 0 and t % 2 == 1), part, parts)

        issued = []
        for step in range(UNITS):
            if step not in issued:
                first_products(step)
                issued.append(step)
            if step + 1 in (3,):
                first_product_grouped(step + 1, half, half)
            nxt = step // GROUPS + 1 if step % GROUPS == 1 and step // GROUPS + 1 < ROUNDS else 0
            x_first = nxt * TILES_PER_ROUND
            if nxt:
                transpose_x(x_first, 2)
                transpose_x(x_first + 2, 2)
            rnd, late = divmod(step - (GROUPS - 1) - SECOND_LAG, GROUPS)
            tiles = []
            if rnd >= 0 and late * TILES_PER_STEP < TILES_PER_ROUND:
                first = rnd * TILES_PER_ROUND + late * TILES_PER_STEP
                tiles = [a for a in range(first, first + TILES_PER_STEP) if a < early_tiles]
            if (step == UNITS - 2) and step + 1 < UNITS:
                first_products(step + 1)
                issued.append(step + 1)
            for a in tiles:
                second_product(a, list(range(GROUPS)))
            if step < UNITS - 1:
                for a in tiles:
                    finish(a)
                if tiles:
                    store(tiles[0], len(tiles))
            if nxt:
                empty_x(x_first, 2, nc.scalar.copy)
                empty_x(x_first + 2, 2, nc.vector.tensor_copy)
            if step in (3,):
                relu(step, half)
                interleave(step, 0, half)
            elif step < UNITS - 1:
                interleave(step)
            if step == 0:
                reorder_w0(2)
                reorder_w0(3)
            if nxt:
                quantise_x(x_first, TILES_PER_ROUND)
            if step - 1 in (3,):
                quantise_h(step - 1, half, half)
                quantise_h(step - 1, 0, half)
            elif step > 0:
                quantise_h(step - 1)

        last = list(range(early_tiles, TOKEN_TILES))
        u = UNITS - 1
        for a in tiles:
            finish(a)
        if tiles:
            store(tiles[0], len(tiles))
        for i in range(1):
            interleave(u, i * P, P)
        for i in range(1, TILES_PER_ROUND):
            interleave(u, i * P, P, nc.scalar.copy)
        for g in range(GROUPS - 1):
            for a in last:
                second_product(a, [g])
        for i, a in enumerate(last):
            quantise_h(u, i * P, P)
        for i, a in enumerate(last):
            second_product(a, [GROUPS - 1])
        for a in last:
            finish(a)
            store(a, 1)
